import numpy as np
import ml_dtypes


def mxq(x, axis, fmt="e4m3"):
    dtype, down = {"e4m3": (ml_dtypes.float8_e4m3fn, 7), "e5m2": (ml_dtypes.float8_e5m2, 14)}[fmt]
    v = np.moveaxis(np.asarray(x, np.float32).astype(ml_dtypes.bfloat16).astype(np.float64), axis, -1)
    blocks = v.reshape(v.shape[:-1] + (-1, 32))
    amax = np.abs(blocks).max(-1, keepdims=True)
    byte = np.maximum(np.where(amax > 0, np.frexp(amax)[1] - 1 + 127, 0) - down, 1)
    scale = np.exp2(byte - 127.0)
    codes = (blocks / scale).astype(np.float32).astype(dtype).astype(np.float64)
    return np.moveaxis((codes * scale).reshape(v.shape), -1, axis)


WIDE = False


def mx_kscale(k):
    if not WIDE:
        return np.ones(k)
    levels = np.array([10, -10, 5, -5, 0])
    a = np.random.permutation(np.resize(levels, k // 512 * 4)).reshape(k // 512, 4)
    idx = np.arange(k)
    return np.exp2(a[idx // 512, idx % 128 // 32])


BF16 = ml_dtypes.bfloat16


def bf(x):
    return np.asarray(x, np.float32).astype(BF16)


def f64(x):
    return np.asarray(x).astype(np.float64)


B, C, E, H, W = 1, 2048, 512, 32, 32
N = H * W
EPS = 1e-5


def setup_inputs():
    t = mx_kscale(E)
    ts = np.sqrt(2.0) / E ** 0.25
    off = np.sign(np.random.standard_normal(E)) * np.random.uniform(1.5, 2.5, E)
    w_bn = np.stack([np.random.uniform(0.5, 1.5, C), np.random.standard_normal(C) * 0.1,
                     np.random.standard_normal(C) * 0.1, np.random.uniform(0.5, 1.5, C)])
    return {"theta": bf(np.random.standard_normal((B, E, N)) * ts),
            "phi": bf(np.random.standard_normal((B, E, N)) * ts),
            "g": bf((np.random.standard_normal((B, E, N)) * 1.5 + off[None, :, None]) * t[None, :, None]),
            "w_w": bf(np.random.standard_normal((C, E)) * 1.2 / np.sqrt(E) / t[None, :]),
            "w_b": bf(np.random.standard_normal(C) * 0.1),
            "w_bn": bf(w_bn),
            "x": bf(np.random.standard_normal((B, C, H, W)))}


def reference(theta, phi, g, w_w, w_b, w_bn, x):
    s = f64(theta).transpose(0, 2, 1) @ f64(phi)
    p = np.exp(s - s.max(-1, keepdims=True))
    y = (mxq(f64(g), 2, "e4m3") @ mxq(p, 2, "e4m3").transpose(0, 2, 1)) / p.sum(-1)[:, None, :]
    z = (mxq(f64(w_w), 1, "e4m3") @ mxq(y, 1, "e4m3")) + f64(w_b)[None, :, None]
    gamma, beta, mean, var = f64(w_bn)
    scale = gamma / np.sqrt(var + EPS)
    out = z * scale[None, :, None] + (beta - mean * scale)[None, :, None]
    return out.reshape(B, C, H, W) + f64(x)

@@ -1,0 +1,278 @@
+from contextlib import ExitStack
+
+import concourse.masks as masks
+import concourse.mybir as mybir
+
+BF16 = mybir.dt.bfloat16
+F32 = mybir.dt.float32
+U32 = mybir.dt.uint32
+U8 = mybir.dt.uint8
+FP8X4 = mybir.dt.float8_e4m3fn_x4
+ALU = mybir.AluOpType
+ACT = mybir.ActivationFunctionType
+AXIS = mybir.AxisListType
+
+P = 128
+EMB = 512
+PIX = 1024
+OUT_CH = 2048
+EPS = 1e-5
+BANK = 512
+EMB_TILES = EMB // P
+ROW_TILES = PIX // P
+OUT_TILES = OUT_CH // P
+HALVES = PIX // BANK
+CHUNK = 2 * P
+CHUNKS = PIX // CHUNK
+BANK_TILES = BANK // CHUNK
+STORE_TILES = 4
+PREP_PER_STEP = 2
+
+FLOPS = 2 * PIX * PIX * EMB * 2 + 2 * OUT_CH * EMB * PIX
+
+
+def by_scalar(bank_index):
+    return bank_index % 3 == 0
+
+
+def rows_to_mx(nc, flip_pool, stage, ident, rows, codes, scales):
+    words = rows.bitcast(F32)
+    flipped = flip_pool.tile([P, BANK], F32, tag="work")
+    for block in range(4):
+        cols = slice(block * P, (block + 1) * P)
+        nc.tensor.transpose(flipped[:, cols], words[:, cols], ident)
+    grouped = stage.tile([P, 2 * BANK], BF16, align_bytes=64)
+    nc.scalar.copy(
+        out=grouped[:].bitcast(F32).rearrange("q (a r u) -> q a r u", a=2, u=2),
+        in_=flipped[:].rearrange("q (a u r) -> q a r u", a=2, u=2),
+    )
+    nc.vector.quantize_mx(out=codes.bitcast(FP8X4), scales=scales, in_=grouped[:])
+
+
+def tile_nonlocalmodule_pa_kernel(tc, theta, phi, g, w_w, w_b, w_bn, x, out):
+    nc = tc.nc
+    with ExitStack() as ctx:
+        keep = ctx.enter_context(tc.tile_pool(name="keep", bufs=1))
+        stage = ctx.enter_context(tc.tile_pool(name="stage", bufs=3))
+        score_pool = ctx.enter_context(tc.psum_pool(name="score_pool", bufs=3))
+        work_pool = ctx.enter_context(tc.psum_pool(name="work_pool", bufs=3))
+        proj_pool = ctx.enter_context(tc.psum_pool(name="proj_pool", bufs=2))
+
+        theta_view = theta[0].rearrange("(p k) n -> p k n", k=EMB_TILES)
+        phi_view = phi[0].rearrange("(p k) m -> p k m", k=EMB_TILES)
+        theta_sb = keep.tile([P, EMB_TILES, PIX], BF16)
+        phi_sb = keep.tile([P, EMB_TILES, PIX], BF16)
+        first, second = slice(0, BANK), slice(BANK, PIX)
+        nc.sync.dma_start(out=theta_sb[:, :, first], in_=theta_view[:, :, first])
+        nc.sync.dma_start(out=phi_sb[:, :, first], in_=phi_view[:, :, first])
+        nc.sync.dma_start(out=phi_sb[:, :, second], in_=phi_view[:, :, second])
+        g_sb = keep.tile([P, EMB_TILES, PIX], BF16)
+        nc.sync.dma_start(
+            out=g_sb[:].rearrange("q (u e) m -> q u (e m)", u=2),
+            in_=g[0].rearrange("(u q e) m -> q u (e m)", u=2, e=2),
+        )
+        w_sb = keep.tile([P, OUT_TILES // 2, 2 * EMB], BF16)
+        w_view = w_w.rearrange("(p a b) c -> p a (b c)", a=OUT_TILES // 2, b=2)
+        for part in range(2):
+            rows = slice(part * 4, (part + 1) * 4)
+            nc.sync.dma_start(out=w_sb[:, rows, :], in_=w_view[:, rows, :])
+        nc.sync.dma_start(out=theta_sb[:, :, second], in_=theta_view[:, :, second])
+        x_sb = keep.tile([P, OUT_TILES, PIX], BF16)
+        x_view = x[0].rearrange("(p j) h w -> p j (h w)", j=OUT_TILES)
+        for part in range(4):
+            rows = slice(part * 4, (part + 1) * 4)
+            nc.sync.dma_start(out=x_sb[:, rows, :], in_=x_view[:, rows, :])
+        out_view = out[0].rearrange("(p j) h w -> p j (h w)", j=OUT_TILES)
+        bn_sb = keep.tile([P, 4, OUT_TILES], BF16)
+        nc.scalar.dma_start(out=bn_sb[:], in_=w_bn.rearrange("v (p j) -> p v j", j=OUT_TILES))
+        wb_sb = keep.tile([P, OUT_TILES], BF16)
+        nc.scalar.dma_start(out=wb_sb[:], in_=w_b.rearrange("(p j) -> p j", j=OUT_TILES))
+
+        ident = keep.tile([P, P], F32)
+        masks.make_identity(nc, ident[:])
+
+        gamma, beta, mean, var = (bn_sb[:, v, :] for v in range(4))
+        var_eps = keep.tile([P, OUT_TILES], F32)
+        nc.vector.tensor_scalar_add(out=var_eps[:], in0=var, scalar1=EPS)
+        std = keep.tile([P, OUT_TILES], F32)
+        nc.scalar.activation(out=std[:], in_=var_eps[:], func=ACT.Sqrt)
+        inv_std = keep.tile([P, OUT_TILES], F32)
+        nc.vector.reciprocal(out=inv_std[:], in_=std[:])
+        scale = keep.tile([P, OUT_TILES], F32)
+        nc.vector.tensor_tensor(out=scale[:], in0=gamma, in1=inv_std[:], op=ALU.mult)
+        centred = keep.tile([P, OUT_TILES], F32)
+        nc.vector.tensor_tensor(out=centred[:], in0=wb_sb[:], in1=mean, op=ALU.subtract)
+        scaled = keep.tile([P, OUT_TILES], F32)
+        nc.vector.tensor_tensor(out=scaled[:], in0=centred[:], in1=scale[:], op=ALU.mult)
+        shift = keep.tile([P, OUT_TILES], F32)
+        nc.vector.tensor_tensor(out=shift[:], in0=scaled[:], in1=beta, op=ALU.add)
+
+        result = keep.tile([P, OUT_TILES, PIX], F32)
+        for j in range(OUT_TILES):
+            if not by_scalar(j // BANK_TILES):
+                nc.gpsimd.tensor_scalar(
+                    out=result[:, j, :],
+                    in0=x_sb[:, j, :],
+                    scalar1=1.0,
+                    scalar2=shift[:, j : j + 1],
+                    op0=ALU.mult,
+                    op1=ALU.add,
+                )
+
+        g_codes = keep.tile([P, EMB_TILES * 2 * P], U32, align_bytes=64)
+        g_scales = keep.tile([P, EMB_TILES * 2 * P], U8, align_bytes=64)
+        w_codes = keep.tile([P, OUT_CH], U32, align_bytes=64)
+        w_scales = keep.tile([P, OUT_CH], U8, align_bytes=64)
+        weight_tiles = []
+        for t in range(EMB_TILES):
+            cols = slice(t * 2 * P, (t + 1) * 2 * P)
+            weight_tiles.append((g_sb[:, t, :], g_codes[:, cols], g_scales[:, cols]))
+        for pair in range(OUT_TILES // 2):
+            cols = slice(pair * 2 * P, (pair + 1) * 2 * P)
+            weight_tiles.append((w_sb[:, pair, :], w_codes[:, cols], w_scales[:, cols]))
+        y_codes = keep.tile([P, PIX], U32, align_bytes=64)
+        y_scales = keep.tile([P, PIX], U8, align_bytes=64)
+
+        prob, inv_sum, p_codes, p_scales, inv_sum_row = {}, {}, {}, {}, {}
+
+        def scores_and_softmax(i):
+            queries = slice(i * P, (i + 1) * P)
+            score = []
+            for half in range(HALVES):
+                keys = slice(half * BANK, (half + 1) * BANK)
+                bank = score_pool.tile([P, BANK], F32, name="score")
+                for k in range(EMB_TILES):
+                    nc.tensor.matmul(
+                        out=bank[:],
+                        lhsT=theta_sb[:, k, queries],
+                        rhs=phi_sb[:, k, keys],
+                        start=(k == 0),
+                        stop=(k == EMB_TILES - 1),
+                    )
+                score.append(bank)
+            half_max = stage.tile([P, HALVES], F32)
+            for half in range(HALVES):
+                nc.vector.tensor_reduce(
+                    out=half_max[:, half : half + 1], in_=score[half][:], axis=AXIS.X, op=ALU.max
+                )
+            neg_max = stage.tile([P, 1], F32)
+            nc.vector.tensor_scalar(
+                out=neg_max[:],
+                in0=half_max[:, 0:1],
+                scalar1=half_max[:, 1:2],
+                scalar2=-1.0,
+                op0=ALU.max,
+                op1=ALU.mult,
+            )
+            prob[i] = stage.tile([P, PIX], BF16, name="prob")
+            half_sum = stage.tile([P, HALVES], F32)
+            for half in range(HALVES):
+                keys = slice(half * BANK, (half + 1) * BANK)
+                nc.scalar.activation(
+                    out=prob[i][:, keys],
+                    in_=score[half][:],
+                    func=ACT.Exp,
+                    bias=neg_max[:, 0:1],
+                    scale=1.0,
+                    accum_out=half_sum[:, half : half + 1],
+                )
+            row_sum = stage.tile([P, 1], F32)
+            nc.vector.tensor_tensor(
+                out=row_sum[:], in0=half_sum[:, 0:1], in1=half_sum[:, 1:2], op=ALU.add
+            )
+            inv_sum[i] = stage.tile([P, 1], F32, name="inv_sum")
+            nc.vector.reciprocal(out=inv_sum[i][:], in_=row_sum[:])
+
+        def flip(i):
+            p_codes[i] = stage.tile([P, 2 * P], U32, align_bytes=64, name="p_codes")
+            p_scales[i] = stage.tile([P, 2 * P], U8, align_bytes=64, name="p_scales")
+            rows_to_mx(nc, work_pool, stage, ident[:], prob[i][:], p_codes[i][:], p_scales[i][:])
+            spread = work_pool.tile([P, P], F32, tag="work")
+            nc.tensor.transpose(spread[:], inv_sum[i][:, 0:1].to_broadcast([P, P]), ident[:])
+            inv_sum_row[i] = stage.tile([P, P], F32, name="inv_sum_row")
+            nc.scalar.copy(out=inv_sum_row[i][:], in_=spread[:])
+
+        def attend(i):
+            queries = slice(i * P, (i + 1) * P)
+            y_ps = work_pool.tile([P, EMB_TILES, P], F32, tag="work")
+            for t in range(EMB_TILES):
+                for a in range(2):
+                    g_cols = slice((2 * t + a) * P, (2 * t + a + 1) * P)
+                    p_cols = slice(a * P, (a + 1) * P)
+                    nc.tensor.matmul_mx(
+                        out=y_ps[:, t, :],
+                        lhsT=g_codes[:, g_cols].bitcast(FP8X4),
+                        lhsT_scale=g_scales[:, g_cols],
+                        rhs=p_codes[i][:, p_cols].bitcast(FP8X4),
+                        rhs_scale=p_scales[i][:, p_cols],
+                        start=(a == 0),
+                        stop=(a == 1),
+                    )
+            y_grouped = stage.tile([P, P, EMB_TILES], BF16, align_bytes=64)
+            nc.vector.tensor_tensor(
+                out=y_grouped[:],
+                in0=y_ps[:].rearrange("q t n -> q n t"),
+                in1=inv_sum_row[i][:].unsqueeze(2).to_broadcast([P, P, EMB_TILES]),
+                op=ALU.mult,
+            )
+            nc.vector.quantize_mx(
+                out=y_codes[:, queries].bitcast(FP8X4),
+                scales=y_scales[:, queries],
+                in_=y_grouped[:].rearrange("q n t -> q (n t)"),
+            )
+
+        def project(chunk, banks):
+            cols = slice(chunk * CHUNK, (chunk + 1) * CHUNK)
+            for bank_index in banks:
+                z_ps = proj_pool.tile([P, BANK_TILES, CHUNK], F32)
+                for b in range(BANK_TILES):
+                    j = bank_index * BANK_TILES + b
+                    w_cols = slice(j * P, (j + 1) * P)
+                    nc.tensor.matmul_mx(
+                        out=z_ps[:, b, :],
+                        lhsT=w_codes[:, w_cols].bitcast(FP8X4),
+                        lhsT_scale=w_scales[:, w_cols],
+                        rhs=y_codes[:, cols].bitcast(FP8X4),
+                        rhs_scale=y_scales[:, cols],
+                        start=True,
+                        stop=True,
+                    )
+                for b in range(BANK_TILES):
+                    j = bank_index * BANK_TILES + b
+                    if by_scalar(bank_index):
+                        nc.scalar.activation(
+                            out=result[:, j, cols],
+                            in_=z_ps[:, b, :],
+                            func=ACT.Identity,
+                            bias=shift[:, j : j + 1],
+                            scale=scale[:, j : j + 1],
+                        )
+                        nc.gpsimd.tensor_tensor(
+                            out=result[:, j, cols], in0=result[:, j, cols], in1=x_sb[:, j, cols], op=ALU.add
+                        )
+                    else:
+                        nc.vector.scalar_tensor_tensor(
+                            out=result[:, j, cols],
+                            in0=z_ps[:, b, :],
+                            scalar=scale[:, j : j + 1],
+                            in1=result[:, j, cols],
+                            op0=ALU.mult,
+                            op1=ALU.add,
+                        )
+                    if j % STORE_TILES == STORE_TILES - 1:
+                        tiles = slice(j + 1 - STORE_TILES, j + 1)
+                        nc.sync.dma_start(out=out_view[:, tiles, cols], in_=result[:, tiles, cols])
+
+        half_banks = OUT_TILES // BANK_TILES // 2
+        for step in range(ROW_TILES + 4):
+            if step < ROW_TILES:
+                scores_and_softmax(step)
+            for rows, codes, scales in weight_tiles[step * PREP_PER_STEP : (step + 1) * PREP_PER_STEP]:
+                rows_to_mx(nc, work_pool, stage, ident[:], rows, codes, scales)
+            if 1 <= step <= ROW_TILES:
+                flip(step - 1)
+            if 2 <= step <= ROW_TILES + 1:
+                attend(step - 2)
+            if step >= 4:
+                part = step % 2
+                project((step - 4) // 2, range(part * half_banks, (part + 1) * half_banks))

@@ -32,21 +32,21 @@ FLOPS = 2 * PIX * PIX * EMB * 2 + 2 * OUT_CH * EMB * PIX
 
 
 def by_scalar(bank_index):
-    return bank_index % 3 == 0
+    return bank_index % 4 == 1
 
 
-def rows_to_mx(nc, flip_pool, stage, ident, rows, codes, scales):
-    words = rows.bitcast(F32)
-    flipped = flip_pool.tile([P, BANK], F32, tag="work")
-    for block in range(4):
-        cols = slice(block * P, (block + 1) * P)
-        nc.tensor.transpose(flipped[:, cols], words[:, cols], ident)
+def flip_block(nc, ident, flipped, rows, block):
+    cols = slice(block * P, (block + 1) * P)
+    nc.tensor.transpose(flipped[:, cols], rows.bitcast(F32)[:, cols], ident)
+
+
+def regroup(nc, stage, flipped):
     grouped = stage.tile([P, 2 * BANK], BF16, align_bytes=64)
     nc.scalar.copy(
         out=grouped[:].bitcast(F32).rearrange("q (a r u) -> q a r u", a=2, u=2),
         in_=flipped[:].rearrange("q (a u r) -> q a r u", a=2, u=2),
     )
-    nc.vector.quantize_mx(out=codes.bitcast(FP8X4), scales=scales, in_=grouped[:])
+    return grouped
 
 
 def tile_nonlocalmodule_pa_kernel(tc, theta, phi, g, w_w, w_b, w_bn, x, out):
@@ -55,7 +55,8 @@ def tile_nonlocalmodule_pa_kernel(tc, theta, phi, g, w_w, w_b, w_bn, x, out):
         keep = ctx.enter_context(tc.tile_pool(name="keep", bufs=1))
         stage = ctx.enter_context(tc.tile_pool(name="stage", bufs=3))
         score_pool = ctx.enter_context(tc.psum_pool(name="score_pool", bufs=3))
-        work_pool = ctx.enter_context(tc.psum_pool(name="work_pool", bufs=3))
+        flip_pool = ctx.enter_context(tc.psum_pool(name="flip_pool", bufs=2))
+        y_pool = ctx.enter_context(tc.psum_pool(name="y_pool", bufs=1))
         proj_pool = ctx.enter_context(tc.psum_pool(name="proj_pool", bufs=2))
 
         theta_view = theta[0].rearrange("(p k) n -> p k n", k=EMB_TILES)
@@ -133,74 +134,82 @@ def tile_nonlocalmodule_pa_kernel(tc, theta, phi, g, w_w, w_b, w_bn, x, out):
         y_codes = keep.tile([P, PIX], U32, align_bytes=64)
         y_scales = keep.tile([P, PIX], U8, align_bytes=64)
 
-        prob, inv_sum, p_codes, p_scales, inv_sum_row = {}, {}, {}, {}, {}
+        score, half_max, neg_max, half_sum, row_sum, inv_sum = {}, {}, {}, {}, {}, {}
+        prob, p_grouped, p_codes, p_scales, inv_sum_row, y_ps, y_grouped = {}, {}, {}, {}, {}, {}, {}
 
-        def scores_and_softmax(i):
+        def scores_half(i, half, rider):
             queries = slice(i * P, (i + 1) * P)
-            score = []
-            for half in range(HALVES):
-                keys = slice(half * BANK, (half + 1) * BANK)
-                bank = score_pool.tile([P, BANK], F32, name="score")
-                for k in range(EMB_TILES):
-                    nc.tensor.matmul(
-                        out=bank[:],
-                        lhsT=theta_sb[:, k, queries],
-                        rhs=phi_sb[:, k, keys],
-                        start=(k == 0),
-                        stop=(k == EMB_TILES - 1),
-                    )
-                score.append(bank)
-            half_max = stage.tile([P, HALVES], F32)
-            for half in range(HALVES):
-                nc.vector.tensor_reduce(
-                    out=half_max[:, half : half + 1], in_=score[half][:], axis=AXIS.X, op=ALU.max
+            keys = slice(half * BANK, (half + 1) * BANK)
+            score[i, half] = score_pool.tile([P, BANK], F32, name="score")
+            for k in range(EMB_TILES):
+                nc.tensor.matmul(
+                    out=score[i, half][:],
+                    lhsT=theta_sb[:, k, queries],
+                    rhs=phi_sb[:, k, keys],
+                    start=(k == 0),
+                    stop=(k == EMB_TILES - 1),
                 )
-            neg_max = stage.tile([P, 1], F32)
+                rider(k)
+
+        def max_half(i, half):
+            if half == 0:
+                half_max[i] = stage.tile([P, HALVES], F32, name="half_max")
+            nc.vector.tensor_reduce(
+                out=half_max[i][:, half : half + 1], in_=score[i, half][:], axis=AXIS.X, op=ALU.max
+            )
+
+        def negate_max(i):
+            neg_max[i] = stage.tile([P, 1], F32, name="neg_max")
             nc.vector.tensor_scalar(
-                out=neg_max[:],
-                in0=half_max[:, 0:1],
-                scalar1=half_max[:, 1:2],
+                out=neg_max[i][:],
+                in0=half_max[i][:, 0:1],
+                scalar1=half_max[i][:, 1:2],
                 scalar2=-1.0,
                 op0=ALU.max,
                 op1=ALU.mult,
             )
+
+        def exponentials(i):
             prob[i] = stage.tile([P, PIX], BF16, name="prob")
-            half_sum = stage.tile([P, HALVES], F32)
+            half_sum[i] = stage.tile([P, HALVES], F32, name="half_sum")
             for half in range(HALVES):
                 keys = slice(half * BANK, (half + 1) * BANK)
                 nc.scalar.activation(
                     out=prob[i][:, keys],
-                    in_=score[half][:],
+                    in_=score[i, half][:],
                     func=ACT.Exp,
-                    bias=neg_max[:, 0:1],
+                    bias=neg_max[i][:, 0:1],
                     scale=1.0,
-                    accum_out=half_sum[:, half : half + 1],
+                    accum_out=half_sum[i][:, half : half + 1],
                 )
-            row_sum = stage.tile([P, 1], F32)
-            nc.vector.tensor_tensor(
-                out=row_sum[:], in0=half_sum[:, 0:1], in1=half_sum[:, 1:2], op=ALU.add
-            )
-            inv_sum[i] = stage.tile([P, 1], F32, name="inv_sum")
-            nc.vector.reciprocal(out=inv_sum[i][:], in_=row_sum[:])
 
-        def flip(i):
-            p_codes[i] = stage.tile([P, 2 * P], U32, align_bytes=64, name="p_codes")
-            p_scales[i] = stage.tile([P, 2 * P], U8, align_bytes=64, name="p_scales")
-            rows_to_mx(nc, work_pool, stage, ident[:], prob[i][:], p_codes[i][:], p_scales[i][:])
-            spread = work_pool.tile([P, P], F32, tag="work")
+        def add_sums(i):
+            row_sum[i] = stage.tile([P, 1], F32, name="row_sum")
+            nc.vector.tensor_tensor(
+                out=row_sum[i][:], in0=half_sum[i][:, 0:1], in1=half_sum[i][:, 1:2], op=ALU.add
+            )
+
+        def invert_sum(i):
+            inv_sum[i] = stage.tile([P, 1], F32, name="inv_sum")
+            nc.vector.reciprocal(out=inv_sum[i][:], in_=row_sum[i][:])
+
+        def spread_inverse(i):
+            spread = flip_pool.tile([P, P], F32, tag="flipped")
             nc.tensor.transpose(spread[:], inv_sum[i][:, 0:1].to_broadcast([P, P]), ident[:])
             inv_sum_row[i] = stage.tile([P, P], F32, name="inv_sum_row")
             nc.scalar.copy(out=inv_sum_row[i][:], in_=spread[:])
 
+        def quantise(grouped, codes, scales):
+            nc.vector.quantize_mx(out=codes.bitcast(FP8X4), scales=scales, in_=grouped[:])
+
         def attend(i):
-            queries = slice(i * P, (i + 1) * P)
-            y_ps = work_pool.tile([P, EMB_TILES, P], F32, tag="work")
+            y_ps[i] = y_pool.tile([P, EMB_TILES, P], F32, name="y_ps")
             for t in range(EMB_TILES):
                 for a in range(2):
                     g_cols = slice((2 * t + a) * P, (2 * t + a + 1) * P)
                     p_cols = slice(a * P, (a + 1) * P)
                     nc.tensor.matmul_mx(
-                        out=y_ps[:, t, :],
+                        out=y_ps[i][:, t, :],
                         lhsT=g_codes[:, g_cols].bitcast(FP8X4),
                         lhsT_scale=g_scales[:, g_cols],
                         rhs=p_codes[i][:, p_cols].bitcast(FP8X4),
@@ -208,71 +217,123 @@ def tile_nonlocalmodule_pa_kernel(tc, theta, phi, g, w_w, w_b, w_bn, x, out):
                         start=(a == 0),
                         stop=(a == 1),
                     )
-            y_grouped = stage.tile([P, P, EMB_TILES], BF16, align_bytes=64)
+
+        def normalise(i):
+            y_grouped[i] = stage.tile([P, P * EMB_TILES], BF16, align_bytes=64, name="y_grouped")
             nc.vector.tensor_tensor(
-                out=y_grouped[:],
-                in0=y_ps[:].rearrange("q t n -> q n t"),
+                out=y_grouped[i][:].rearrange("q (n t) -> q n t", t=EMB_TILES),
+                in0=y_ps[i][:].rearrange("q t n -> q n t"),
                 in1=inv_sum_row[i][:].unsqueeze(2).to_broadcast([P, P, EMB_TILES]),
                 op=ALU.mult,
             )
-            nc.vector.quantize_mx(
-                out=y_codes[:, queries].bitcast(FP8X4),
-                scales=y_scales[:, queries],
-                in_=y_grouped[:].rearrange("q n t -> q (n t)"),
-            )
 
-        def project(chunk, banks):
+        def project(chunk, bank_index):
             cols = slice(chunk * CHUNK, (chunk + 1) * CHUNK)
-            for bank_index in banks:
-                z_ps = proj_pool.tile([P, BANK_TILES, CHUNK], F32)
-                for b in range(BANK_TILES):
-                    j = bank_index * BANK_TILES + b
-                    w_cols = slice(j * P, (j + 1) * P)
-                    nc.tensor.matmul_mx(
-                        out=z_ps[:, b, :],
-                        lhsT=w_codes[:, w_cols].bitcast(FP8X4),
-                        lhsT_scale=w_scales[:, w_cols],
-                        rhs=y_codes[:, cols].bitcast(FP8X4),
-                        rhs_scale=y_scales[:, cols],
-                        start=True,
-                        stop=True,
+            z_ps = proj_pool.tile([P, BANK_TILES, CHUNK], F32)
+            for b in range(BANK_TILES):
+                j = bank_index * BANK_TILES + b
+                w_cols = slice(j * P, (j + 1) * P)
+                nc.tensor.matmul_mx(
+                    out=z_ps[:, b, :],
+                    lhsT=w_codes[:, w_cols].bitcast(FP8X4),
+                    lhsT_scale=w_scales[:, w_cols],
+                    rhs=y_codes[:, cols].bitcast(FP8X4),
+                    rhs_scale=y_scales[:, cols],
+                    start=True,
+                    stop=True,
+                )
+            for b in range(BANK_TILES):
+                j = bank_index * BANK_TILES + b
+                if by_scalar(bank_index):
+                    nc.scalar.activation(
+                        out=result[:, j, cols],
+                        in_=z_ps[:, b, :],
+                        func=ACT.Identity,
+                        bias=shift[:, j : j + 1],
+                        scale=scale[:, j : j + 1],
                     )
-                for b in range(BANK_TILES):
-                    j = bank_index * BANK_TILES + b
-                    if by_scalar(bank_index):
-                        nc.scalar.activation(
-                            out=result[:, j, cols],
-                            in_=z_ps[:, b, :],
-                            func=ACT.Identity,
-                            bias=shift[:, j : j + 1],
-                            scale=scale[:, j : j + 1],
-                        )
-                        nc.gpsimd.tensor_tensor(
-                            out=result[:, j, cols], in0=result[:, j, cols], in1=x_sb[:, j, cols], op=ALU.add
-                        )
-                    else:
-                        nc.vector.scalar_tensor_tensor(
-                            out=result[:, j, cols],
-                            in0=z_ps[:, b, :],
-                            scalar=scale[:, j : j + 1],
-                            in1=result[:, j, cols],
-                            op0=ALU.mult,
-                            op1=ALU.add,
-                        )
-                    if j % STORE_TILES == STORE_TILES - 1:
-                        tiles = slice(j + 1 - STORE_TILES, j + 1)
-                        nc.sync.dma_start(out=out_view[:, tiles, cols], in_=result[:, tiles, cols])
+                else:
+                    nc.vector.scalar_tensor_tensor(
+                        out=result[:, j, cols],
+                        in0=z_ps[:, b, :],
+                        scalar=scale[:, j : j + 1],
+                        in1=result[:, j, cols],
+                        op0=ALU.mult,
+                        op1=ALU.add,
+                    )
+            last = bank_index * BANK_TILES + BANK_TILES
+            if by_scalar(bank_index):
+                pair = slice(last - BANK_TILES, last)
+                nc.gpsimd.tensor_tensor(
+                    out=result[:, pair, cols], in0=result[:, pair, cols], in1=x_sb[:, pair, cols], op=ALU.add
+                )
+            if last % STORE_TILES == 0:
+                tiles = slice(last - STORE_TILES, last)
+                nc.sync.dma_start(out=out_view[:, tiles, cols], in_=result[:, tiles, cols])
 
-        half_banks = OUT_TILES // BANK_TILES // 2
-        for step in range(ROW_TILES + 4):
-            if step < ROW_TILES:
-                scores_and_softmax(step)
-            for rows, codes, scales in weight_tiles[step * PREP_PER_STEP : (step + 1) * PREP_PER_STEP]:
-                rows_to_mx(nc, work_pool, stage, ident[:], rows, codes, scales)
-            if 1 <= step <= ROW_TILES:
-                flip(step - 1)
-            if 2 <= step <= ROW_TILES + 1:
+        step_banks = OUT_TILES // BANK_TILES // 2
+        ctx.enter_context(tc.manual_schedule())
+        for step in range(ROW_TILES + 5):
+            scoring = step < ROW_TILES
+            flipping = 1 <= step <= ROW_TILES
+            attending = 2 <= step <= ROW_TILES + 1
+            projecting = step >= 5
+            chunk = (step - 5) // 2
+            first_bank = ((step - 5) % 2) * step_banks
+            weights = weight_tiles[max(step - 1, 0) * PREP_PER_STEP : step * PREP_PER_STEP]
+
+            if flipping:
+                add_sums(step - 1)
+            w_flipped = []
+            for n in range(len(weights)):
+                w_flipped.append(flip_pool.tile([P, BANK], F32, tag="flipped", name="w_flipped"))
+
+            def weight_rider(k):
+                for (rows, codes, scales), flipped in zip(weights, w_flipped):
+                    flip_block(nc, ident[:], flipped, rows, k)
+
+            if scoring:
+                scores_half(step, 0, weight_rider)
+            w_grouped = [regroup(nc, stage, flipped) for flipped in w_flipped]
+            if scoring:
+                max_half(step, 0)
+            if flipping:
+                invert_sum(step - 1)
+            for (rows, codes, scales), grouped in zip(weights, w_grouped):
+                quantise(grouped, codes, scales)
+            if attending:
                 attend(step - 2)
-            if step >= 4:
-                part = step % 2
-                project((step - 4) // 2, range(part * half_banks, (part + 1) * half_banks))
+                normalise(step - 2)
+            if projecting:
+                project(chunk, first_bank)
+                project(chunk, first_bank + 1)
+            if attending:
+                queries = slice((step - 2) * P, (step - 1) * P)
+                quantise(y_grouped[step - 2], y_codes[:, queries], y_scales[:, queries])
+
+            if flipping:
+                p_flipped = flip_pool.tile([P, BANK], F32, tag="flipped")
+
+            def prob_rider(k):
+                if flipping:
+                    flip_block(nc, ident[:], p_flipped, prob[step - 1][:], k)
+
+            if scoring:
+                scores_half(step, 1, prob_rider)
+            else:
+                for k in range(EMB_TILES):
+                    prob_rider(k)
+            if flipping:
+                p_grouped[step - 1] = regroup(nc, stage, p_flipped)
+                spread_inverse(step - 1)
+            if scoring:
+                max_half(step, 1)
+                negate_max(step)
+                exponentials(step)
+            if projecting:
+                project(chunk, first_bank + 2)
+                project(chunk, first_bank + 3)
+            if flipping:
+                p_codes[step - 1] = stage.tile([P, 2 * P], U32, align_bytes=64, name="p_codes")
+                p_scales[step - 1] = stage.tile([P, 2 * P], U8, align_bytes=64, name="p_scales")
+                quantise(p_grouped[step - 1], p_codes[step - 1][:], p_scales[step - 1][:])

@@ -32,21 +32,21 @@ FLOPS = 2 * PIX * PIX * EMB * 2 + 2 * OUT_CH * EMB * PIX
 
 
 def by_scalar(bank_index):
-    return bank_index % 4 == 1
+    return bank_index % 4 == 0
 
 
-def flip_block(nc, ident, flipped, rows, block):
-    cols = slice(block * P, (block + 1) * P)
-    nc.tensor.transpose(flipped[:, cols], rows.bitcast(F32)[:, cols], ident)
-
-
-def regroup(nc, stage, flipped):
+def rows_to_mx(nc, flip_pool, stage, ident, rows, codes, scales):
+    words = rows.bitcast(F32)
+    flipped = flip_pool.tile([P, BANK], F32, tag="bank")
+    for block in range(4):
+        cols = slice(block * P, (block + 1) * P)
+        nc.tensor.transpose(flipped[:, cols], words[:, cols], ident)
     grouped = stage.tile([P, 2 * BANK], BF16, align_bytes=64)
     nc.scalar.copy(
         out=grouped[:].bitcast(F32).rearrange("q (a r u) -> q a r u", a=2, u=2),
         in_=flipped[:].rearrange("q (a u r) -> q a r u", a=2, u=2),
     )
-    return grouped
+    nc.vector.quantize_mx(out=codes.bitcast(FP8X4), scales=scales, in_=grouped[:])
 
 
 def tile_nonlocalmodule_pa_kernel(tc, theta, phi, g, w_w, w_b, w_bn, x, out):
@@ -54,18 +54,16 @@ def tile_nonlocalmodule_pa_kernel(tc, theta, phi, g, w_w, w_b, w_bn, x, out):
     with ExitStack() as ctx:
         keep = ctx.enter_context(tc.tile_pool(name="keep", bufs=1))
         stage = ctx.enter_context(tc.tile_pool(name="stage", bufs=3))
-        score_pool = ctx.enter_context(tc.psum_pool(name="score_pool", bufs=3))
-        flip_pool = ctx.enter_context(tc.psum_pool(name="flip_pool", bufs=2))
-        y_pool = ctx.enter_context(tc.psum_pool(name="y_pool", bufs=1))
-        proj_pool = ctx.enter_context(tc.psum_pool(name="proj_pool", bufs=2))
+        psum = ctx.enter_context(tc.psum_pool(name="psum", bufs=8))
 
         theta_view = theta[0].rearrange("(p k) n -> p k n", k=EMB_TILES)
         phi_view = phi[0].rearrange("(p k) m -> p k m", k=EMB_TILES)
         theta_sb = keep.tile([P, EMB_TILES, PIX], BF16)
         phi_sb = keep.tile([P, EMB_TILES, PIX], BF16)
         first, second = slice(0, BANK), slice(BANK, PIX)
-        nc.sync.dma_start(out=theta_sb[:, :, first], in_=theta_view[:, :, first])
-        nc.sync.dma_start(out=phi_sb[:, :, first], in_=phi_view[:, :, first])
+        for slots in (slice(0, 2), slice(2, 4)):
+            nc.sync.dma_start(out=theta_sb[:, slots, first], in_=theta_view[:, slots, first])
+            nc.sync.dma_start(out=phi_sb[:, slots, first], in_=phi_view[:, slots, first])
         nc.sync.dma_start(out=phi_sb[:, :, second], in_=phi_view[:, :, second])
         g_sb = keep.tile([P, EMB_TILES, PIX], BF16)
         nc.sync.dma_start(
@@ -134,82 +132,74 @@ def tile_nonlocalmodule_pa_kernel(tc, theta, phi, g, w_w, w_b, w_bn, x, out):
         y_codes = keep.tile([P, PIX], U32, align_bytes=64)
         y_scales = keep.tile([P, PIX], U8, align_bytes=64)
 
-        score, half_max, neg_max, half_sum, row_sum, inv_sum = {}, {}, {}, {}, {}, {}
-        prob, p_grouped, p_codes, p_scales, inv_sum_row, y_ps, y_grouped = {}, {}, {}, {}, {}, {}, {}
+        prob, inv_sum, p_codes, p_scales, inv_sum_row = {}, {}, {}, {}, {}
 
-        def scores_half(i, half, rider):
+        def scores_and_softmax(i):
             queries = slice(i * P, (i + 1) * P)
-            keys = slice(half * BANK, (half + 1) * BANK)
-            score[i, half] = score_pool.tile([P, BANK], F32, name="score")
-            for k in range(EMB_TILES):
-                nc.tensor.matmul(
-                    out=score[i, half][:],
-                    lhsT=theta_sb[:, k, queries],
-                    rhs=phi_sb[:, k, keys],
-                    start=(k == 0),
-                    stop=(k == EMB_TILES - 1),
+            score = []
+            for half in range(HALVES):
+                keys = slice(half * BANK, (half + 1) * BANK)
+                bank = psum.tile([P, BANK], F32, name="score", tag="bank")
+                for k in range(EMB_TILES):
+                    nc.tensor.matmul(
+                        out=bank[:],
+                        lhsT=theta_sb[:, k, queries],
+                        rhs=phi_sb[:, k, keys],
+                        start=(k == 0),
+                        stop=(k == EMB_TILES - 1),
+                    )
+                score.append(bank)
+            half_max = stage.tile([P, HALVES], F32)
+            for half in range(HALVES):
+                nc.vector.tensor_reduce(
+                    out=half_max[:, half : half + 1], in_=score[half][:], axis=AXIS.X, op=ALU.max
                 )
-                rider(k)
-
-        def max_half(i, half):
-            if half == 0:
-                half_max[i] = stage.tile([P, HALVES], F32, name="half_max")
-            nc.vector.tensor_reduce(
-                out=half_max[i][:, half : half + 1], in_=score[i, half][:], axis=AXIS.X, op=ALU.max
-            )
-
-        def negate_max(i):
-            neg_max[i] = stage.tile([P, 1], F32, name="neg_max")
+            neg_max = stage.tile([P, 1], F32)
             nc.vector.tensor_scalar(
-                out=neg_max[i][:],
-                in0=half_max[i][:, 0:1],
-                scalar1=half_max[i][:, 1:2],
+                out=neg_max[:],
+                in0=half_max[:, 0:1],
+                scalar1=half_max[:, 1:2],
                 scalar2=-1.0,
                 op0=ALU.max,
                 op1=ALU.mult,
             )
-
-        def exponentials(i):
             prob[i] = stage.tile([P, PIX], BF16, name="prob")
-            half_sum[i] = stage.tile([P, HALVES], F32, name="half_sum")
+            half_sum = stage.tile([P, HALVES], F32)
             for half in range(HALVES):
                 keys = slice(half * BANK, (half + 1) * BANK)
                 nc.scalar.activation(
                     out=prob[i][:, keys],
-                    in_=score[i, half][:],
+                    in_=score[half][:],
                     func=ACT.Exp,
-                    bias=neg_max[i][:, 0:1],
+                    bias=neg_max[:, 0:1],
                     scale=1.0,
-                    accum_out=half_sum[i][:, half : half + 1],
+                    accum_out=half_sum[:, half : half + 1],
                 )
-
-        def add_sums(i):
-            row_sum[i] = stage.tile([P, 1], F32, name="row_sum")
+            row_sum = stage.tile([P, 1], F32)
             nc.vector.tensor_tensor(
-                out=row_sum[i][:], in0=half_sum[i][:, 0:1], in1=half_sum[i][:, 1:2], op=ALU.add
+                out=row_sum[:], in0=half_sum[:, 0:1], in1=half_sum[:, 1:2], op=ALU.add
             )
-
-        def invert_sum(i):
             inv_sum[i] = stage.tile([P, 1], F32, name="inv_sum")
-            nc.vector.reciprocal(out=inv_sum[i][:], in_=row_sum[i][:])
+            nc.vector.reciprocal(out=inv_sum[i][:], in_=row_sum[:])
 
-        def spread_inverse(i):
-            spread = flip_pool.tile([P, P], F32, tag="flipped")
+        def flip(i):
+            p_codes[i] = stage.tile([P, 2 * P], U32, align_bytes=64, name="p_codes")
+            p_scales[i] = stage.tile([P, 2 * P], U8, align_bytes=64, name="p_scales")
+            rows_to_mx(nc, psum, stage, ident[:], prob[i][:], p_codes[i][:], p_scales[i][:])
+            spread = psum.tile([P, P], F32, tag="bank")
             nc.tensor.transpose(spread[:], inv_sum[i][:, 0:1].to_broadcast([P, P]), ident[:])
             inv_sum_row[i] = stage.tile([P, P], F32, name="inv_sum_row")
             nc.scalar.copy(out=inv_sum_row[i][:], in_=spread[:])
 
-        def quantise(grouped, codes, scales):
-            nc.vector.quantize_mx(out=codes.bitcast(FP8X4), scales=scales, in_=grouped[:])
-
         def attend(i):
-            y_ps[i] = y_pool.tile([P, EMB_TILES, P], F32, name="y_ps")
+            queries = slice(i * P, (i + 1) * P)
+            y_ps = psum.tile([P, EMB_TILES, P], F32, tag="bank")
             for t in range(EMB_TILES):
                 for a in range(2):
                     g_cols = slice((2 * t + a) * P, (2 * t + a + 1) * P)
                     p_cols = slice(a * P, (a + 1) * P)
                     nc.tensor.matmul_mx(
-                        out=y_ps[i][:, t, :],
+                        out=y_ps[:, t, :],
                         lhsT=g_codes[:, g_cols].bitcast(FP8X4),
                         lhsT_scale=g_scales[:, g_cols],
                         rhs=p_codes[i][:, p_cols].bitcast(FP8X4),
@@ -217,123 +207,74 @@ def tile_nonlocalmodule_pa_kernel(tc, theta, phi, g, w_w, w_b, w_bn, x, out):
                         start=(a == 0),
                         stop=(a == 1),
                     )
-
-        def normalise(i):
-            y_grouped[i] = stage.tile([P, P * EMB_TILES], BF16, align_bytes=64, name="y_grouped")
+            y_grouped = stage.tile([P, P, EMB_TILES], BF16, align_bytes=64)
             nc.vector.tensor_tensor(
-                out=y_grouped[i][:].rearrange("q (n t) -> q n t", t=EMB_TILES),
-                in0=y_ps[i][:].rearrange("q t n -> q n t"),
+                out=y_grouped[:],
+                in0=y_ps[:].rearrange("q t n -> q n t"),
                 in1=inv_sum_row[i][:].unsqueeze(2).to_broadcast([P, P, EMB_TILES]),
                 op=ALU.mult,
             )
+            nc.vector.quantize_mx(
+                out=y_codes[:, queries].bitcast(FP8X4),
+                scales=y_scales[:, queries],
+                in_=y_grouped[:].rearrange("q n t -> q (n t)"),
+            )
 
-        def project(chunk, bank_index):
+        def project(chunk, banks):
             cols = slice(chunk * CHUNK, (chunk + 1) * CHUNK)
-            z_ps = proj_pool.tile([P, BANK_TILES, CHUNK], F32)
-            for b in range(BANK_TILES):
-                j = bank_index * BANK_TILES + b
-                w_cols = slice(j * P, (j + 1) * P)
-                nc.tensor.matmul_mx(
-                    out=z_ps[:, b, :],
-                    lhsT=w_codes[:, w_cols].bitcast(FP8X4),
-                    lhsT_scale=w_scales[:, w_cols],
-                    rhs=y_codes[:, cols].bitcast(FP8X4),
-                    rhs_scale=y_scales[:, cols],
-                    start=True,
-                    stop=True,
-                )
-            for b in range(BANK_TILES):
-                j = bank_index * BANK_TILES + b
+            for bank_index in banks:
+                z_ps = psum.tile([P, BANK_TILES, CHUNK], F32, tag="bank")
+                for b in range(BANK_TILES):
+                    j = bank_index * BANK_TILES + b
+                    w_cols = slice(j * P, (j + 1) * P)
+                    nc.tensor.matmul_mx(
+                        out=z_ps[:, b, :],
+                        lhsT=w_codes[:, w_cols].bitcast(FP8X4),
+                        lhsT_scale=w_scales[:, w_cols],
+                        rhs=y_codes[:, cols].bitcast(FP8X4),
+                        rhs_scale=y_scales[:, cols],
+                        start=True,
+                        stop=True,
+                    )
+                for b in range(BANK_TILES):
+                    j = bank_index * BANK_TILES + b
+                    if by_scalar(bank_index):
+                        nc.scalar.activation(
+                            out=result[:, j, cols],
+                            in_=z_ps[:, b, :],
+                            func=ACT.Identity,
+                            bias=shift[:, j : j + 1],
+                            scale=scale[:, j : j + 1],
+                        )
+                    else:
+                        nc.vector.scalar_tensor_tensor(
+                            out=result[:, j, cols],
+                            in0=z_ps[:, b, :],
+                            scalar=scale[:, j : j + 1],
+                            in1=result[:, j, cols],
+                            op0=ALU.mult,
+                            op1=ALU.add,
+                        )
+                last = (bank_index + 1) * BANK_TILES
                 if by_scalar(bank_index):
-                    nc.scalar.activation(
-                        out=result[:, j, cols],
-                        in_=z_ps[:, b, :],
-                        func=ACT.Identity,
-                        bias=shift[:, j : j + 1],
-                        scale=scale[:, j : j + 1],
+                    pair = slice(last - BANK_TILES, last)
+                    nc.gpsimd.tensor_tensor(
+                        out=result[:, pair, cols], in0=result[:, pair, cols], in1=x_sb[:, pair, cols], op=ALU.add
                     )
-                else:
-                    nc.vector.scalar_tensor_tensor(
-                        out=result[:, j, cols],
-                        in0=z_ps[:, b, :],
-                        scalar=scale[:, j : j + 1],
-                        in1=result[:, j, cols],
-                        op0=ALU.mult,
-                        op1=ALU.add,
-                    )
-            last = bank_index * BANK_TILES + BANK_TILES
-            if by_scalar(bank_index):
-                pair = slice(last - BANK_TILES, last)
-                nc.gpsimd.tensor_tensor(
-                    out=result[:, pair, cols], in0=result[:, pair, cols], in1=x_sb[:, pair, cols], op=ALU.add
-                )
-            if last % STORE_TILES == 0:
-                tiles = slice(last - STORE_TILES, last)
-                nc.sync.dma_start(out=out_view[:, tiles, cols], in_=result[:, tiles, cols])
+                if last % STORE_TILES == 0:
+                    tiles = slice(last - STORE_TILES, last)
+                    nc.sync.dma_start(out=out_view[:, tiles, cols], in_=result[:, tiles, cols])
 
-        step_banks = OUT_TILES // BANK_TILES // 2
-        ctx.enter_context(tc.manual_schedule())
-        for step in range(ROW_TILES + 5):
-            scoring = step < ROW_TILES
-            flipping = 1 <= step <= ROW_TILES
-            attending = 2 <= step <= ROW_TILES + 1
-            projecting = step >= 5
-            chunk = (step - 5) // 2
-            first_bank = ((step - 5) % 2) * step_banks
-            weights = weight_tiles[max(step - 1, 0) * PREP_PER_STEP : step * PREP_PER_STEP]
-
-            if flipping:
-                add_sums(step - 1)
-            w_flipped = []
-            for n in range(len(weights)):
-                w_flipped.append(flip_pool.tile([P, BANK], F32, tag="flipped", name="w_flipped"))
-
-            def weight_rider(k):
-                for (rows, codes, scales), flipped in zip(weights, w_flipped):
-                    flip_block(nc, ident[:], flipped, rows, k)
-
-            if scoring:
-                scores_half(step, 0, weight_rider)
-            w_grouped = [regroup(nc, stage, flipped) for flipped in w_flipped]
-            if scoring:
-                max_half(step, 0)
-            if flipping:
-                invert_sum(step - 1)
-            for (rows, codes, scales), grouped in zip(weights, w_grouped):
-                quantise(grouped, codes, scales)
-            if attending:
+        half_banks = OUT_TILES // BANK_TILES // 2
+        for step in range(ROW_TILES + 4):
+            if step < ROW_TILES:
+                scores_and_softmax(step)
+            for rows, codes, scales in weight_tiles[step * PREP_PER_STEP : (step + 1) * PREP_PER_STEP]:
+                rows_to_mx(nc, psum, stage, ident[:], rows, codes, scales)
+            if 1 <= step <= ROW_TILES:
+                flip(step - 1)
+            if 2 <= step <= ROW_TILES + 1:
                 attend(step - 2)
-                normalise(step - 2)
-            if projecting:
-                project(chunk, first_bank)
-                project(chunk, first_bank + 1)
-            if attending:
-                queries = slice((step - 2) * P, (step - 1) * P)
-                quantise(y_grouped[step - 2], y_codes[:, queries], y_scales[:, queries])
-
-            if flipping:
-                p_flipped = flip_pool.tile([P, BANK], F32, tag="flipped")
-
-            def prob_rider(k):
-                if flipping:
-                    flip_block(nc, ident[:], p_flipped, prob[step - 1][:], k)
-
-            if scoring:
-                scores_half(step, 1, prob_rider)
-            else:
-                for k in range(EMB_TILES):
-                    prob_rider(k)
-            if flipping:
-                p_grouped[step - 1] = regroup(nc, stage, p_flipped)
-                spread_inverse(step - 1)
-            if scoring:
-                max_half(step, 1)
-                negate_max(step)
-                exponentials(step)
-            if projecting:
-                project(chunk, first_bank + 2)
-                project(chunk, first_bank + 3)
-            if flipping:
-                p_codes[step - 1] = stage.tile([P, 2 * P], U32, align_bytes=64, name="p_codes")
-                p_scales[step - 1] = stage.tile([P, 2 * P], U8, align_bytes=64, name="p_scales")
-                quantise(p_grouped[step - 1], p_codes[step - 1][:], p_scales[step - 1][:])
+            if step >= 4:
+                part = step % 2
+                project((step - 4) // 2, range(part * half_banks, (part + 1) * half_banks))

@@ -25,36 +25,23 @@ HALVES = PIX // BANK
 CHUNK = 2 * P
 CHUNKS = PIX // CHUNK
 BANK_TILES = BANK // CHUNK
+HALF_BANKS = OUT_TILES // BANK_TILES // 2
 STORE_TILES = 4
-PREP_PER_STEP = 2
 
 FLOPS = 2 * PIX * PIX * EMB * 2 + 2 * OUT_CH * EMB * PIX
 
 
 def by_scalar(bank_index):
-    return bank_index % 4 == 0
-
-
-def rows_to_mx(nc, flip_pool, stage, ident, rows, codes, scales):
-    words = rows.bitcast(F32)
-    flipped = flip_pool.tile([P, BANK], F32, tag="bank")
-    for block in range(4):
-        cols = slice(block * P, (block + 1) * P)
-        nc.tensor.transpose(flipped[:, cols], words[:, cols], ident)
-    grouped = stage.tile([P, 2 * BANK], BF16, align_bytes=64)
-    nc.scalar.copy(
-        out=grouped[:].bitcast(F32).rearrange("q (a r u) -> q a r u", a=2, u=2),
-        in_=flipped[:].rearrange("q (a u r) -> q a r u", a=2, u=2),
-    )
-    nc.vector.quantize_mx(out=codes.bitcast(FP8X4), scales=scales, in_=grouped[:])
+    return bank_index % HALF_BANKS == 0
 
 
 def tile_nonlocalmodule_pa_kernel(tc, theta, phi, g, w_w, w_b, w_bn, x, out):
     nc = tc.nc
     with ExitStack() as ctx:
         keep = ctx.enter_context(tc.tile_pool(name="keep", bufs=1))
-        stage = ctx.enter_context(tc.tile_pool(name="stage", bufs=3))
-        psum = ctx.enter_context(tc.psum_pool(name="psum", bufs=8))
+        stage = ctx.enter_context(tc.tile_pool(name="stage", bufs=4))
+        score_psum = ctx.enter_context(tc.psum_pool(name="score_psum", bufs=3))
+        psum = ctx.enter_context(tc.psum_pool(name="psum", bufs=5))
 
         theta_view = theta[0].rearrange("(p k) n -> p k n", k=EMB_TILES)
         phi_view = phi[0].rearrange("(p k) m -> p k m", k=EMB_TILES)
@@ -66,22 +53,30 @@ def tile_nonlocalmodule_pa_kernel(tc, theta, phi, g, w_w, w_b, w_bn, x, out):
             nc.sync.dma_start(out=phi_sb[:, slots, first], in_=phi_view[:, slots, first])
         nc.sync.dma_start(out=phi_sb[:, :, second], in_=phi_view[:, :, second])
         g_sb = keep.tile([P, EMB_TILES, PIX], BF16)
-        nc.sync.dma_start(
-            out=g_sb[:].rearrange("q (u e) m -> q u (e m)", u=2),
-            in_=g[0].rearrange("(u q e) m -> q u (e m)", u=2, e=2),
-        )
+        g_view = g[0].rearrange("(t q) m -> q t m", q=P)
         w_sb = keep.tile([P, OUT_TILES // 2, 2 * EMB], BF16)
         w_view = w_w.rearrange("(p a b) c -> p a (b c)", a=OUT_TILES // 2, b=2)
-        for part in range(2):
-            rows = slice(part * 4, (part + 1) * 4)
-            nc.sync.dma_start(out=w_sb[:, rows, :], in_=w_view[:, rows, :])
-        nc.sync.dma_start(out=theta_sb[:, :, second], in_=theta_view[:, :, second])
         x_sb = keep.tile([P, OUT_TILES, PIX], BF16)
         x_view = x[0].rearrange("(p j) h w -> p j (h w)", j=OUT_TILES)
-        for part in range(4):
+        out_view = out[0].rearrange("(p j) h w -> p j (h w)", j=OUT_TILES)
+
+        def load_w(part):
+            rows = slice(part * 4, (part + 1) * 4)
+            nc.sync.dma_start(out=w_sb[:, rows, :], in_=w_view[:, rows, :])
+
+        def load_x(part):
             rows = slice(part * 4, (part + 1) * 4)
             nc.sync.dma_start(out=x_sb[:, rows, :], in_=x_view[:, rows, :])
-        out_view = out[0].rearrange("(p j) h w -> p j (h w)", j=OUT_TILES)
+
+        for pair in (slice(0, 2), slice(2, 4)):
+            nc.sync.dma_start(out=g_sb[:, pair, :], in_=g_view[:, pair, :])
+        load_x(0)
+        load_x(1)
+        load_w(0)
+        load_w(1)
+        nc.sync.dma_start(out=theta_sb[:, :, second], in_=theta_view[:, :, second])
+        load_x(2)
+        load_x(3)
         bn_sb = keep.tile([P, 4, OUT_TILES], BF16)
         nc.scalar.dma_start(out=bn_sb[:], in_=w_bn.rearrange("v (p j) -> p v j", j=OUT_TILES))
         wb_sb = keep.tile([P, OUT_TILES], BF16)
@@ -89,135 +84,140 @@ def tile_nonlocalmodule_pa_kernel(tc, theta, phi, g, w_w, w_b, w_bn, x, out):
 
         ident = keep.tile([P, P], F32)
         masks.make_identity(nc, ident[:])
+        warm = keep.tile([P, 1], F32)
+        nc.vector.memset(warm[:], 0.0)
+        warm_out = keep.tile([P, 1], F32)
+        nc.scalar.activation(out=warm_out[:], in_=warm[:], func=ACT.Exp)
 
         gamma, beta, mean, var = (bn_sb[:, v, :] for v in range(4))
+        minus_half = keep.tile([P, OUT_TILES], F32)
+        nc.gpsimd.memset(minus_half[:], -0.5)
         var_eps = keep.tile([P, OUT_TILES], F32)
         nc.vector.tensor_scalar_add(out=var_eps[:], in0=var, scalar1=EPS)
-        std = keep.tile([P, OUT_TILES], F32)
-        nc.scalar.activation(out=std[:], in_=var_eps[:], func=ACT.Sqrt)
         inv_std = keep.tile([P, OUT_TILES], F32)
-        nc.vector.reciprocal(out=inv_std[:], in_=std[:])
-        scale = keep.tile([P, OUT_TILES], F32)
-        nc.vector.tensor_tensor(out=scale[:], in0=gamma, in1=inv_std[:], op=ALU.mult)
+        nc.gpsimd.tensor_tensor(out=inv_std[:], in0=var_eps[:], in1=minus_half[:], op=ALU.pow)
         centred = keep.tile([P, OUT_TILES], F32)
         nc.vector.tensor_tensor(out=centred[:], in0=wb_sb[:], in1=mean, op=ALU.subtract)
+        scale = keep.tile([P, OUT_TILES], F32)
+        nc.vector.tensor_tensor(out=scale[:], in0=gamma, in1=inv_std[:], op=ALU.mult)
         scaled = keep.tile([P, OUT_TILES], F32)
         nc.vector.tensor_tensor(out=scaled[:], in0=centred[:], in1=scale[:], op=ALU.mult)
         shift = keep.tile([P, OUT_TILES], F32)
         nc.vector.tensor_tensor(out=shift[:], in0=scaled[:], in1=beta, op=ALU.add)
 
         result = keep.tile([P, OUT_TILES, PIX], F32)
-        for j in range(OUT_TILES):
-            if not by_scalar(j // BANK_TILES):
-                nc.gpsimd.tensor_scalar(
-                    out=result[:, j, :],
-                    in0=x_sb[:, j, :],
-                    scalar1=1.0,
-                    scalar2=shift[:, j : j + 1],
-                    op0=ALU.mult,
-                    op1=ALU.add,
-                )
-
-        g_codes = keep.tile([P, EMB_TILES * 2 * P], U32, align_bytes=64)
-        g_scales = keep.tile([P, EMB_TILES * 2 * P], U8, align_bytes=64)
+        g_codes = keep.tile([P, 2 * EMB], U32, align_bytes=64)
+        g_scales = keep.tile([P, 2 * EMB], U8, align_bytes=64)
         w_codes = keep.tile([P, OUT_CH], U32, align_bytes=64)
         w_scales = keep.tile([P, OUT_CH], U8, align_bytes=64)
-        weight_tiles = []
-        for t in range(EMB_TILES):
-            cols = slice(t * 2 * P, (t + 1) * 2 * P)
-            weight_tiles.append((g_sb[:, t, :], g_codes[:, cols], g_scales[:, cols]))
-        for pair in range(OUT_TILES // 2):
-            cols = slice(pair * 2 * P, (pair + 1) * 2 * P)
-            weight_tiles.append((w_sb[:, pair, :], w_codes[:, cols], w_scales[:, cols]))
         y_codes = keep.tile([P, PIX], U32, align_bytes=64)
         y_scales = keep.tile([P, PIX], U8, align_bytes=64)
 
-        prob, inv_sum, p_codes, p_scales, inv_sum_row = {}, {}, {}, {}, {}
-
-        def scores_and_softmax(i):
-            queries = slice(i * P, (i + 1) * P)
-            score = []
-            for half in range(HALVES):
-                keys = slice(half * BANK, (half + 1) * BANK)
-                bank = psum.tile([P, BANK], F32, name="score", tag="bank")
-                for k in range(EMB_TILES):
-                    nc.tensor.matmul(
-                        out=bank[:],
-                        lhsT=theta_sb[:, k, queries],
-                        rhs=phi_sb[:, k, keys],
-                        start=(k == 0),
-                        stop=(k == EMB_TILES - 1),
-                    )
-                score.append(bank)
-            half_max = stage.tile([P, HALVES], F32)
-            for half in range(HALVES):
-                nc.vector.tensor_reduce(
-                    out=half_max[:, half : half + 1], in_=score[half][:], axis=AXIS.X, op=ALU.max
-                )
-            neg_max = stage.tile([P, 1], F32)
-            nc.vector.tensor_scalar(
-                out=neg_max[:],
-                in0=half_max[:, 0:1],
-                scalar1=half_max[:, 1:2],
-                scalar2=-1.0,
-                op0=ALU.max,
-                op1=ALU.mult,
+        def flip_to_mx(blocks, codes, scales, copy):
+            groups = len(blocks) // 2
+            width = len(blocks) * P
+            flipped = psum.tile([P, width], F32, tag="bank", name="flipped")
+            for b, block in enumerate(blocks):
+                nc.tensor.transpose(flipped[:, b * P : (b + 1) * P], block, ident[:])
+            grouped = stage.tile([P, 2 * width], BF16, align_bytes=64, name="grouped", tag="grouped%d" % groups)
+            copy(
+                out=grouped[:].bitcast(F32).rearrange("q (a r u) -> q a r u", a=groups, u=2),
+                in_=flipped[:].rearrange("q (a u r) -> q a r u", a=groups, u=2),
             )
+            nc.vector.quantize_mx(out=codes.bitcast(FP8X4), scales=scales, in_=grouped[:])
+
+        def words_of(rows, count):
+            words = rows.bitcast(F32)
+            return [words[:, b * P : (b + 1) * P] for b in range(count)]
+
+        def flip_g(a, pair, copy):
+            blocks = []
+            for t in (2 * pair, 2 * pair + 1):
+                blocks.extend(words_of(g_sb[:, t, :], 4)[2 * a : 2 * a + 2])
+            cols = slice(a * EMB + pair * 2 * P, a * EMB + (pair + 1) * 2 * P)
+            flip_to_mx(blocks, g_codes[:, cols], g_scales[:, cols], copy)
+
+        def flip_w(pair, copy):
+            cols = slice(pair * 2 * P, (pair + 1) * 2 * P)
+            flip_to_mx(words_of(w_sb[:, pair, :], 4), w_codes[:, cols], w_scales[:, cols], copy)
+
+        score, neg_max, prob, half_sum, inv_sum = {}, {}, {}, {}, {}
+        p_codes, p_scales, y_rows = {}, {}, {}
+
+        def scores(i, half):
+            queries = slice(i * P, (i + 1) * P)
+            keys = slice(half * BANK, (half + 1) * BANK)
+            score[i, half] = score_psum.tile([P, BANK], F32, name="score")
+            for k in range(EMB_TILES):
+                nc.tensor.matmul(
+                    out=score[i, half][:],
+                    lhsT=theta_sb[:, k, queries],
+                    rhs=phi_sb[:, k, keys],
+                    start=(k == 0),
+                    stop=(k == EMB_TILES - 1),
+                )
+            negated = stage.tile([P, BANK], BF16, name="negated")
+            neg_max[i, half] = stage.tile([P, 1], F32, name="neg_max%d" % half)
+            nc.vector.tensor_scalar(
+                out=negated[:],
+                in0=score[i, half][:],
+                scalar1=-1.0,
+                scalar2=None if half == 0 else neg_max[i, 0][:, 0:1],
+                op0=ALU.mult,
+                op1=ALU.min,
+                accum_out=neg_max[i, half][:, 0:1],
+            )
+
+        def softmax(i):
             prob[i] = stage.tile([P, PIX], BF16, name="prob")
-            half_sum = stage.tile([P, HALVES], F32)
+            half_sum[i] = stage.tile([P, HALVES], F32, name="half_sum")
             for half in range(HALVES):
                 keys = slice(half * BANK, (half + 1) * BANK)
                 nc.scalar.activation(
                     out=prob[i][:, keys],
-                    in_=score[half][:],
+                    in_=score[i, half][:],
                     func=ACT.Exp,
-                    bias=neg_max[:, 0:1],
+                    bias=neg_max[i, 1][:, 0:1],
                     scale=1.0,
-                    accum_out=half_sum[:, half : half + 1],
+                    accum_out=half_sum[i][:, half : half + 1],
                 )
+
+        def invert_sum(i):
             row_sum = stage.tile([P, 1], F32)
-            nc.vector.tensor_tensor(
-                out=row_sum[:], in0=half_sum[:, 0:1], in1=half_sum[:, 1:2], op=ALU.add
-            )
+            nc.vector.tensor_reduce(out=row_sum[:], in_=half_sum[i][:], axis=AXIS.X, op=ALU.add)
             inv_sum[i] = stage.tile([P, 1], F32, name="inv_sum")
             nc.vector.reciprocal(out=inv_sum[i][:], in_=row_sum[:])
 
-        def flip(i):
+        def flip_p(i):
             p_codes[i] = stage.tile([P, 2 * P], U32, align_bytes=64, name="p_codes")
             p_scales[i] = stage.tile([P, 2 * P], U8, align_bytes=64, name="p_scales")
-            rows_to_mx(nc, psum, stage, ident[:], prob[i][:], p_codes[i][:], p_scales[i][:])
-            spread = psum.tile([P, P], F32, tag="bank")
-            nc.tensor.transpose(spread[:], inv_sum[i][:, 0:1].to_broadcast([P, P]), ident[:])
-            inv_sum_row[i] = stage.tile([P, P], F32, name="inv_sum_row")
-            nc.scalar.copy(out=inv_sum_row[i][:], in_=spread[:])
+            flip_to_mx(words_of(prob[i][:], 4), p_codes[i][:], p_scales[i][:], nc.scalar.copy)
 
         def attend(i):
-            queries = slice(i * P, (i + 1) * P)
-            y_ps = psum.tile([P, EMB_TILES, P], F32, tag="bank")
-            for t in range(EMB_TILES):
-                for a in range(2):
-                    g_cols = slice((2 * t + a) * P, (2 * t + a + 1) * P)
-                    p_cols = slice(a * P, (a + 1) * P)
-                    nc.tensor.matmul_mx(
-                        out=y_ps[:, t, :],
-                        lhsT=g_codes[:, g_cols].bitcast(FP8X4),
-                        lhsT_scale=g_scales[:, g_cols],
-                        rhs=p_codes[i][:, p_cols].bitcast(FP8X4),
-                        rhs_scale=p_scales[i][:, p_cols],
-                        start=(a == 0),
-                        stop=(a == 1),
-                    )
-            y_grouped = stage.tile([P, P, EMB_TILES], BF16, align_bytes=64)
-            nc.vector.tensor_tensor(
-                out=y_grouped[:],
-                in0=y_ps[:].rearrange("q t n -> q n t"),
-                in1=inv_sum_row[i][:].unsqueeze(2).to_broadcast([P, P, EMB_TILES]),
-                op=ALU.mult,
-            )
-            nc.vector.quantize_mx(
-                out=y_codes[:, queries].bitcast(FP8X4),
-                scales=y_scales[:, queries],
-                in_=y_grouped[:].rearrange("q n t -> q (n t)"),
+            y_ps = psum.tile([P, EMB], F32, tag="bank")
+            for a in range(2):
+                p_cols = slice(a * P, (a + 1) * P)
+                g_cols = slice(a * EMB, (a + 1) * EMB)
+                nc.tensor.matmul_mx(
+                    out=y_ps[:],
+                    lhsT=p_codes[i][:, p_cols].bitcast(FP8X4),
+                    lhsT_scale=p_scales[i][:, p_cols],
+                    rhs=g_codes[:, g_cols].bitcast(FP8X4),
+                    rhs_scale=g_scales[:, g_cols],
+                    start=(a == 0),
+                    stop=(a == 1),
+                )
+            y_rows[i] = stage.tile([P, EMB], BF16, name="y_rows")
+            nc.scalar.activation(out=y_rows[i][:], in_=y_ps[:], func=ACT.Copy, scale=inv_sum[i][:, 0:1])
+
+        def flip_y(i):
+            cols = slice(i * P, (i + 1) * P)
+            flip_to_mx(words_of(y_rows[i][:], 2), y_codes[:, cols], y_scales[:, cols], nc.scalar.copy)
+
+        def add_shift(engine, j):
+            engine.tensor_scalar(
+                out=result[:, j, :], in0=x_sb[:, j, :], scalar1=1.0, scalar2=shift[:, j : j + 1],
+                op0=ALU.mult, op1=ALU.add,
             )
 
         def project(chunk, banks):
@@ -265,16 +265,40 @@ def tile_nonlocalmodule_pa_kernel(tc, theta, phi, g, w_w, w_b, w_bn, x, out):
                     tiles = slice(last - STORE_TILES, last)
                     nc.sync.dma_start(out=out_view[:, tiles, cols], in_=result[:, tiles, cols])
 
-        half_banks = OUT_TILES // BANK_TILES // 2
-        for step in range(ROW_TILES + 4):
-            if step < ROW_TILES:
-                scores_and_softmax(step)
-            for rows, codes, scales in weight_tiles[step * PREP_PER_STEP : (step + 1) * PREP_PER_STEP]:
-                rows_to_mx(nc, psum, stage, ident[:], rows, codes, scales)
-            if 1 <= step <= ROW_TILES:
-                flip(step - 1)
-            if 2 <= step <= ROW_TILES + 1:
-                attend(step - 2)
-            if step >= 4:
-                part = step % 2
-                project((step - 4) // 2, range(part * half_banks, (part + 1) * half_banks))
+        flips_mid = {
+            1: [(flip_g, (1, 0)), (flip_g, (1, 1))],
+            2: [(flip_w, (0,)), (flip_w, (1,))],
+            3: [(flip_w, (2,)), (flip_w, (3,)), (flip_w, (4,))],
+            4: [(flip_w, (5,)), (flip_w, (6,)), (flip_w, (7,))],
+        }
+        flips_end = {0: [(flip_g, (0, 0)), (flip_g, (0, 1))]}
+        gpsimd_shift = {1: (2, 3), 2: (4, 5, 6, 7), 3: (10, 11), 4: (12, 13, 14, 15)}
+        with tc.manual_schedule():
+            for step in range(ROW_TILES + 2):
+                if 1 <= step <= ROW_TILES:
+                    invert_sum(step - 1)
+                if step < ROW_TILES:
+                    scores(step, 0)
+                if 1 <= step <= ROW_TILES:
+                    flip_p(step - 1)
+                if 2 <= step:
+                    flip_y(step - 2)
+                for flip, args in flips_mid.get(step, []):
+                    flip(*args, nc.scalar.copy)
+                if step < ROW_TILES:
+                    scores(step, 1)
+                for j in gpsimd_shift.get(step, ()):
+                    add_shift(nc.gpsimd, j)
+                half = (step - 3) % 2
+                chunk = (step - 3) // 2
+                if 3 <= step:
+                    project(chunk, range(half * HALF_BANKS, half * HALF_BANKS + 1))
+                if step < ROW_TILES:
+                    softmax(step)
+                for flip, args in flips_end.get(step, []):
+                    flip(*args, nc.scalar.copy)
+                if 3 <= step:
+                    project(chunk, range(half * HALF_BANKS + 1, (half + 1) * HALF_BANKS))
+                if 1 <= step <= ROW_TILES:
+                    attend(step - 1)
+            project(CHUNKS - 1, range(HALF_BANKS, 2 * HALF_BANKS))

@@ -22,17 +22,15 @@ EMB_TILES = EMB // P
 ROW_TILES = PIX // P
 OUT_TILES = OUT_CH // P
 HALVES = PIX // BANK
-CHUNK = 2 * P
-CHUNKS = PIX // CHUNK
-BANK_TILES = BANK // CHUNK
-HALF_BANKS = OUT_TILES // BANK_TILES // 2
+PAIR = 2 * P
 STORE_TILES = 4
+WARM_PASSES = 6
 
 FLOPS = 2 * PIX * PIX * EMB * 2 + 2 * OUT_CH * EMB * PIX
 
 
-def by_scalar(bank_index):
-    return bank_index % HALF_BANKS == 0
+def by_scalar(j, width):
+    return j % 8 < 2
 
 
 def tile_nonlocalmodule_pa_kernel(tc, theta, phi, g, w_w, w_b, w_bn, x, out):
@@ -50,10 +48,9 @@ def tile_nonlocalmodule_pa_kernel(tc, theta, phi, g, w_w, w_b, w_bn, x, out):
         first, second = slice(0, BANK), slice(BANK, PIX)
         for slots in (slice(0, 2), slice(2, 4)):
             nc.sync.dma_start(out=theta_sb[:, slots, first], in_=theta_view[:, slots, first])
-            nc.sync.dma_start(out=phi_sb[:, slots, first], in_=phi_view[:, slots, first])
-        nc.sync.dma_start(out=phi_sb[:, :, second], in_=phi_view[:, :, second])
+            nc.sync.dma_start(out=phi_sb[:, slots, :], in_=phi_view[:, slots, :])
         g_sb = keep.tile([P, EMB_TILES, PIX], BF16)
-        g_view = g[0].rearrange("(t q) m -> q t m", q=P)
+        g_view = g[0].rearrange("(u q e) m -> q u (e m)", u=2, e=2)
         w_sb = keep.tile([P, OUT_TILES // 2, 2 * EMB], BF16)
         w_view = w_w.rearrange("(p a b) c -> p a (b c)", a=OUT_TILES // 2, b=2)
         x_sb = keep.tile([P, OUT_TILES, PIX], BF16)
@@ -68,11 +65,11 @@ def tile_nonlocalmodule_pa_kernel(tc, theta, phi, g, w_w, w_b, w_bn, x, out):
             rows = slice(part * 4, (part + 1) * 4)
             nc.sync.dma_start(out=x_sb[:, rows, :], in_=x_view[:, rows, :])
 
-        for pair in (slice(0, 2), slice(2, 4)):
-            nc.sync.dma_start(out=g_sb[:, pair, :], in_=g_view[:, pair, :])
+        for u in range(2):
+            nc.sync.dma_start(out=g_sb[:, 2 * u : 2 * u + 2, :].rearrange("q e m -> q (e m)"), in_=g_view[:, u, :])
+        load_w(0)
         load_x(0)
         load_x(1)
-        load_w(0)
         load_w(1)
         nc.sync.dma_start(out=theta_sb[:, :, second], in_=theta_view[:, :, second])
         load_x(2)
@@ -88,6 +85,11 @@ def tile_nonlocalmodule_pa_kernel(tc, theta, phi, g, w_w, w_b, w_bn, x, out):
         nc.vector.memset(warm[:], 0.0)
         warm_out = keep.tile([P, 1], F32)
         nc.scalar.activation(out=warm_out[:], in_=warm[:], func=ACT.Exp)
+        zeros = keep.tile([P, BANK], BF16)
+        nc.vector.memset(zeros[:], 0.0)
+        idle = psum.tile([P, BANK], F32, tag="bank")
+        for n in range(WARM_PASSES):
+            nc.tensor.matmul(out=idle[:], lhsT=zeros[:, 0:P], rhs=zeros[:], start=True, stop=True)
 
         gamma, beta, mean, var = (bn_sb[:, v, :] for v in range(4))
         minus_half = keep.tile([P, OUT_TILES], F32)
@@ -113,7 +115,7 @@ def tile_nonlocalmodule_pa_kernel(tc, theta, phi, g, w_w, w_b, w_bn, x, out):
         y_codes = keep.tile([P, PIX], U32, align_bytes=64)
         y_scales = keep.tile([P, PIX], U8, align_bytes=64)
 
-        def flip_to_mx(blocks, codes, scales, copy):
+        def flip_to_mx(blocks, codes, scales, copy, order="a r u"):
             groups = len(blocks) // 2
             width = len(blocks) * P
             flipped = psum.tile([P, width], F32, tag="bank", name="flipped")
@@ -121,8 +123,8 @@ def tile_nonlocalmodule_pa_kernel(tc, theta, phi, g, w_w, w_b, w_bn, x, out):
                 nc.tensor.transpose(flipped[:, b * P : (b + 1) * P], block, ident[:])
             grouped = stage.tile([P, 2 * width], BF16, align_bytes=64, name="grouped", tag="grouped%d" % groups)
             copy(
-                out=grouped[:].bitcast(F32).rearrange("q (a r u) -> q a r u", a=groups, u=2),
-                in_=flipped[:].rearrange("q (a u r) -> q a r u", a=groups, u=2),
+                out=grouped[:].bitcast(F32).rearrange("q (%s) -> q %s" % (order, order), a=groups, u=2),
+                in_=flipped[:].rearrange("q (a u r) -> q %s" % order, a=groups, u=2),
             )
             nc.vector.quantize_mx(out=codes.bitcast(FP8X4), scales=scales, in_=grouped[:])
 
@@ -135,7 +137,7 @@ def tile_nonlocalmodule_pa_kernel(tc, theta, phi, g, w_w, w_b, w_bn, x, out):
             for t in (2 * pair, 2 * pair + 1):
                 blocks.extend(words_of(g_sb[:, t, :], 4)[2 * a : 2 * a + 2])
             cols = slice(a * EMB + pair * 2 * P, a * EMB + (pair + 1) * 2 * P)
-            flip_to_mx(blocks, g_codes[:, cols], g_scales[:, cols], copy)
+            flip_to_mx(blocks, g_codes[:, cols], g_scales[:, cols], copy, "r a u")
 
         def flip_w(pair, copy):
             cols = slice(pair * 2 * P, (pair + 1) * 2 * P)
@@ -144,11 +146,12 @@ def tile_nonlocalmodule_pa_kernel(tc, theta, phi, g, w_w, w_b, w_bn, x, out):
         score, neg_max, prob, half_sum, inv_sum = {}, {}, {}, {}, {}
         p_codes, p_scales, y_rows = {}, {}, {}
 
-        def scores(i, half):
+        def score_passes(i, half, slots):
             queries = slice(i * P, (i + 1) * P)
             keys = slice(half * BANK, (half + 1) * BANK)
-            score[i, half] = score_psum.tile([P, BANK], F32, name="score")
-            for k in range(EMB_TILES):
+            if slots[0] == 0:
+                score[i, half] = score_psum.tile([P, BANK], F32, name="score")
+            for k in slots:
                 nc.tensor.matmul(
                     out=score[i, half][:],
                     lhsT=theta_sb[:, k, queries],
@@ -156,6 +159,8 @@ def tile_nonlocalmodule_pa_kernel(tc, theta, phi, g, w_w, w_b, w_bn, x, out):
                     start=(k == 0),
                     stop=(k == EMB_TILES - 1),
                 )
+
+        def score_max(i, half):
             negated = stage.tile([P, BANK], BF16, name="negated")
             neg_max[i, half] = stage.tile([P, 1], F32, name="neg_max%d" % half)
             nc.vector.tensor_scalar(
@@ -167,6 +172,10 @@ def tile_nonlocalmodule_pa_kernel(tc, theta, phi, g, w_w, w_b, w_bn, x, out):
                 op1=ALU.min,
                 accum_out=neg_max[i, half][:, 0:1],
             )
+
+        def scores(i, half):
+            score_passes(i, half, range(EMB_TILES))
+            score_max(i, half)
 
         def softmax(i):
             prob[i] = stage.tile([P, PIX], BF16, name="prob")
@@ -214,19 +223,19 @@ def tile_nonlocalmodule_pa_kernel(tc, theta, phi, g, w_w, w_b, w_bn, x, out):
             cols = slice(i * P, (i + 1) * P)
             flip_to_mx(words_of(y_rows[i][:], 2), y_codes[:, cols], y_scales[:, cols], nc.scalar.copy)
 
-        def add_shift(engine, j):
+        def add_shift(engine, j, cols):
             engine.tensor_scalar(
-                out=result[:, j, :], in0=x_sb[:, j, :], scalar1=1.0, scalar2=shift[:, j : j + 1],
+                out=result[:, j, cols], in0=x_sb[:, j, cols], scalar1=1.0, scalar2=shift[:, j : j + 1],
                 op0=ALU.mult, op1=ALU.add,
             )
 
-        def project(chunk, banks):
-            cols = slice(chunk * CHUNK, (chunk + 1) * CHUNK)
-            for bank_index in banks:
-                z_ps = psum.tile([P, BANK_TILES, CHUNK], F32, tag="bank")
-                for b in range(BANK_TILES):
-                    j = bank_index * BANK_TILES + b
-                    w_cols = slice(j * P, (j + 1) * P)
+        def project(start, width, tiles, store_from=None):
+            cols = slice(start, start + width)
+            per_bank = BANK // width
+            for j0 in range(tiles[0], tiles[1], per_bank):
+                z_ps = psum.tile([P, per_bank, width], F32, tag="bank", name="z_ps")
+                for b in range(per_bank):
+                    w_cols = slice((j0 + b) * P, (j0 + b + 1) * P)
                     nc.tensor.matmul_mx(
                         out=z_ps[:, b, :],
                         lhsT=w_codes[:, w_cols].bitcast(FP8X4),
@@ -236,9 +245,9 @@ def tile_nonlocalmodule_pa_kernel(tc, theta, phi, g, w_w, w_b, w_bn, x, out):
                         start=True,
                         stop=True,
                     )
-                for b in range(BANK_TILES):
-                    j = bank_index * BANK_TILES + b
-                    if by_scalar(bank_index):
+                for b in range(per_bank):
+                    j = j0 + b
+                    if by_scalar(j, width):
                         nc.scalar.activation(
                             out=result[:, j, cols],
                             in_=z_ps[:, b, :],
@@ -255,50 +264,133 @@ def tile_nonlocalmodule_pa_kernel(tc, theta, phi, g, w_w, w_b, w_bn, x, out):
                             op0=ALU.mult,
                             op1=ALU.add,
                         )
-                last = (bank_index + 1) * BANK_TILES
-                if by_scalar(bank_index):
-                    pair = slice(last - BANK_TILES, last)
+                if by_scalar(j0, width):
+                    bank_tiles = slice(j0, j0 + 2)
                     nc.gpsimd.tensor_tensor(
-                        out=result[:, pair, cols], in0=result[:, pair, cols], in1=x_sb[:, pair, cols], op=ALU.add
+                        out=result[:, bank_tiles, cols],
+                        in0=result[:, bank_tiles, cols],
+                        in1=x_sb[:, bank_tiles, cols],
+                        op=ALU.add,
                     )
-                if last % STORE_TILES == 0:
-                    tiles = slice(last - STORE_TILES, last)
-                    nc.sync.dma_start(out=out_view[:, tiles, cols], in_=result[:, tiles, cols])
+                last = j0 + per_bank
+                if store_from is not None and last % STORE_TILES == 0:
+                    stored = slice(last - STORE_TILES, last)
+                    done = slice(store_from, start + width)
+                    nc.sync.dma_start(out=out_view[:, stored, done], in_=result[:, stored, done])
 
-        flips_mid = {
-            1: [(flip_g, (1, 0)), (flip_g, (1, 1))],
-            2: [(flip_w, (0,)), (flip_w, (1,))],
-            3: [(flip_w, (2,)), (flip_w, (3,)), (flip_w, (4,))],
-            4: [(flip_w, (5,)), (flip_w, (6,)), (flip_w, (7,))],
-        }
-        flips_end = {0: [(flip_g, (0, 0)), (flip_g, (0, 1))]}
-        gpsimd_shift = {1: (2, 3), 2: (4, 5, 6, 7), 3: (10, 11), 4: (12, 13, 14, 15)}
         with tc.manual_schedule():
-            for step in range(ROW_TILES + 2):
-                if 1 <= step <= ROW_TILES:
-                    invert_sum(step - 1)
-                if step < ROW_TILES:
-                    scores(step, 0)
-                if 1 <= step <= ROW_TILES:
-                    flip_p(step - 1)
-                if 2 <= step:
-                    flip_y(step - 2)
-                for flip, args in flips_mid.get(step, []):
-                    flip(*args, nc.scalar.copy)
-                if step < ROW_TILES:
-                    scores(step, 1)
-                for j in gpsimd_shift.get(step, ()):
-                    add_shift(nc.gpsimd, j)
-                half = (step - 3) % 2
-                chunk = (step - 3) // 2
-                if 3 <= step:
-                    project(chunk, range(half * HALF_BANKS, half * HALF_BANKS + 1))
-                if step < ROW_TILES:
-                    softmax(step)
-                for flip, args in flips_end.get(step, []):
-                    flip(*args, nc.scalar.copy)
-                if 3 <= step:
-                    project(chunk, range(half * HALF_BANKS + 1, (half + 1) * HALF_BANKS))
-                if 1 <= step <= ROW_TILES:
-                    attend(step - 1)
-            project(CHUNKS - 1, range(HALF_BANKS, 2 * HALF_BANKS))
+            for slots in ((0, 1), (2, 3)):
+                for half in range(HALVES):
+                    score_passes(0, half, slots)
+            for half in range(HALVES):
+                score_max(0, half)
+            softmax(0)
+            flip_g(0, 0, nc.scalar.copy)
+            flip_g(0, 1, nc.scalar.copy)
+            invert_sum(0)
+            scores(1, 0)
+            flip_p(0)
+            flip_g(1, 0, nc.scalar.copy)
+            flip_g(1, 1, nc.scalar.copy)
+            scores(1, 1)
+            add_shift(nc.gpsimd, 2, slice(0, 1024))
+            add_shift(nc.gpsimd, 3, slice(0, 1024))
+            softmax(1)
+            flip_w(0, nc.vector.tensor_copy)
+            flip_w(1, nc.vector.tensor_copy)
+            attend(0)
+            invert_sum(1)
+            scores(2, 0)
+            flip_p(1)
+            flip_y(0)
+            scores(2, 1)
+            add_shift(nc.gpsimd, 4, slice(0, 1024))
+            add_shift(nc.gpsimd, 5, slice(0, 1024))
+            add_shift(nc.gpsimd, 6, slice(0, 1024))
+            add_shift(nc.gpsimd, 7, slice(0, 1024))
+            softmax(2)
+            flip_w(2, nc.vector.tensor_copy)
+            flip_w(3, nc.vector.tensor_copy)
+            attend(1)
+            invert_sum(2)
+            scores(3, 0)
+            flip_p(2)
+            flip_y(1)
+            flip_w(4, nc.scalar.copy)
+            flip_w(5, nc.scalar.copy)
+            scores(3, 1)
+            add_shift(nc.gpsimd, 10, slice(0, 1024))
+            add_shift(nc.gpsimd, 11, slice(0, 1024))
+            project(0, 256, (0, 2), 0)
+            softmax(3)
+            project(0, 256, (2, 4), 0)
+            project(0, 256, (4, 6), 0)
+            project(0, 256, (6, 8), 0)
+            attend(2)
+            invert_sum(3)
+            scores(4, 0)
+            flip_p(3)
+            flip_y(2)
+            flip_w(6, nc.scalar.copy)
+            flip_w(7, nc.scalar.copy)
+            scores(4, 1)
+            add_shift(nc.gpsimd, 12, slice(0, 1024))
+            add_shift(nc.gpsimd, 13, slice(0, 1024))
+            add_shift(nc.gpsimd, 14, slice(0, 1024))
+            add_shift(nc.gpsimd, 15, slice(0, 1024))
+            project(0, 256, (8, 10), 0)
+            softmax(4)
+            project(0, 256, (10, 12), 0)
+            project(0, 256, (12, 14), 0)
+            project(0, 256, (14, 16), 0)
+            attend(3)
+            invert_sum(4)
+            scores(5, 0)
+            flip_p(4)
+            flip_y(3)
+            scores(5, 1)
+            project(256, 256, (0, 2), 256)
+            softmax(5)
+            project(256, 256, (2, 4), 256)
+            project(256, 256, (4, 6), 256)
+            project(256, 256, (6, 8), 256)
+            attend(4)
+            invert_sum(5)
+            scores(6, 0)
+            flip_p(5)
+            flip_y(4)
+            scores(6, 1)
+            project(256, 256, (8, 10), 256)
+            softmax(6)
+            project(256, 256, (10, 12), 256)
+            project(256, 256, (12, 14), 256)
+            project(256, 256, (14, 16), 256)
+            attend(5)
+            invert_sum(6)
+            scores(7, 0)
+            flip_p(6)
+            flip_y(5)
+            scores(7, 1)
+            project(512, 256, (0, 2), 512)
+            softmax(7)
+            project(512, 256, (2, 4), 512)
+            project(512, 256, (4, 6), 512)
+            project(512, 256, (6, 8), 512)
+            attend(6)
+            project(512, 256, (8, 10), 512)
+            project(512, 256, (10, 12), 512)
+            invert_sum(7)
+            flip_p(7)
+            flip_y(6)
+            project(512, 256, (12, 14), 512)
+            project(512, 256, (14, 16), 512)
+            attend(7)
+            project(768, 128, (0, 4), 768)
+            project(768, 128, (4, 8), 768)
+            project(768, 128, (8, 12), 768)
+            flip_y(7)
+            project(768, 128, (12, 16), 768)
+            project(896, 128, (0, 4), 896)
+            project(896, 128, (4, 8), 896)
+            project(896, 128, (8, 12), 896)
+            project(896, 128, (12, 16), 896)

@@ -45,10 +45,9 @@ def tile_nonlocalmodule_pa_kernel(tc, theta, phi, g, w_w, w_b, w_bn, x, out):
         phi_view = phi[0].rearrange("(p k) m -> p k m", k=EMB_TILES)
         theta_sb = keep.tile([P, EMB_TILES, PIX], BF16)
         phi_sb = keep.tile([P, EMB_TILES, PIX], BF16)
-        first, second = slice(0, BANK), slice(BANK, PIX)
-        for slots in (slice(0, 2), slice(2, 4)):
-            nc.sync.dma_start(out=theta_sb[:, slots, first], in_=theta_view[:, slots, first])
-            nc.sync.dma_start(out=phi_sb[:, slots, :], in_=phi_view[:, slots, :])
+        nc.sync.dma_start(out=theta_sb[:, :, 0:PAIR], in_=theta_view[:, :, 0:PAIR])
+        for k in range(EMB_TILES):
+            nc.sync.dma_start(out=phi_sb[:, k, :], in_=phi_view[:, k, :])
         g_sb = keep.tile([P, EMB_TILES, PIX], BF16)
         g_view = g[0].rearrange("(u q e) m -> q u (e m)", u=2, e=2)
         w_sb = keep.tile([P, OUT_TILES // 2, 2 * EMB], BF16)
@@ -67,11 +66,12 @@ def tile_nonlocalmodule_pa_kernel(tc, theta, phi, g, w_w, w_b, w_bn, x, out):
 
         for u in range(2):
             nc.sync.dma_start(out=g_sb[:, 2 * u : 2 * u + 2, :].rearrange("q e m -> q (e m)"), in_=g_view[:, u, :])
+        nc.sync.dma_start(out=theta_sb[:, :, 256:512], in_=theta_view[:, :, 256:512])
         load_w(0)
         load_x(0)
         load_x(1)
         load_w(1)
-        nc.sync.dma_start(out=theta_sb[:, :, second], in_=theta_view[:, :, second])
+        nc.sync.dma_start(out=theta_sb[:, :, 512:1024], in_=theta_view[:, :, 512:1024])
         load_x(2)
         load_x(3)
         bn_sb = keep.tile([P, 4, OUT_TILES], BF16)
@@ -224,10 +224,19 @@ def tile_nonlocalmodule_pa_kernel(tc, theta, phi, g, w_w, w_b, w_bn, x, out):
             flip_to_mx(words_of(y_rows[i][:], 2), y_codes[:, cols], y_scales[:, cols], nc.scalar.copy)
 
         def add_shift(engine, j, cols):
-            engine.tensor_scalar(
-                out=result[:, j, cols], in0=x_sb[:, j, cols], scalar1=1.0, scalar2=shift[:, j : j + 1],
-                op0=ALU.mult, op1=ALU.add,
-            )
+            if engine is nc.scalar:
+                nc.scalar.activation(
+                    out=result[:, j, cols], in_=x_sb[:, j, cols], func=ACT.Identity, bias=shift[:, j : j + 1], scale=1.0
+                )
+            else:
+                engine.tensor_scalar(
+                    out=result[:, j, cols],
+                    in0=x_sb[:, j, cols],
+                    scalar1=1.0,
+                    scalar2=shift[:, j : j + 1],
+                    op0=ALU.mult,
+                    op1=ALU.add,
+                )
 
         def project(start, width, tiles, store_from=None):
             cols = slice(start, start + width)
@@ -279,116 +288,116 @@ def tile_nonlocalmodule_pa_kernel(tc, theta, phi, g, w_w, w_b, w_bn, x, out):
                     nc.sync.dma_start(out=out_view[:, stored, done], in_=result[:, stored, done])
 
         with tc.manual_schedule():
-            for slots in ((0, 1), (2, 3)):
+            for k in range(EMB_TILES):
                 for half in range(HALVES):
-                    score_passes(0, half, slots)
+                    score_passes(0, half, (k,))
             for half in range(HALVES):
                 score_max(0, half)
-            softmax(0)
             flip_g(0, 0, nc.scalar.copy)
-            flip_g(0, 1, nc.scalar.copy)
+            softmax(0)
             invert_sum(0)
             scores(1, 0)
-            flip_p(0)
-            flip_g(1, 0, nc.scalar.copy)
+            flip_g(0, 1, nc.scalar.copy)
             flip_g(1, 1, nc.scalar.copy)
             scores(1, 1)
-            add_shift(nc.gpsimd, 2, slice(0, 1024))
-            add_shift(nc.gpsimd, 3, slice(0, 1024))
-            softmax(1)
+            flip_g(1, 0, nc.scalar.copy)
+            flip_p(0)
             flip_w(0, nc.vector.tensor_copy)
-            flip_w(1, nc.vector.tensor_copy)
-            attend(0)
-            invert_sum(1)
             scores(2, 0)
+            softmax(1)
+            attend(0)
+            add_shift(nc.gpsimd, 2, slice(0, 1024))
+            invert_sum(1)
+            scores(2, 1)
             flip_p(1)
             flip_y(0)
-            scores(2, 1)
+            flip_w(1, nc.vector.tensor_copy)
+            add_shift(nc.gpsimd, 3, slice(0, 1024))
+            scores(3, 0)
+            softmax(2)
+            attend(1)
             add_shift(nc.gpsimd, 4, slice(0, 1024))
             add_shift(nc.gpsimd, 5, slice(0, 1024))
-            add_shift(nc.gpsimd, 6, slice(0, 1024))
-            add_shift(nc.gpsimd, 7, slice(0, 1024))
-            softmax(2)
             flip_w(2, nc.vector.tensor_copy)
-            flip_w(3, nc.vector.tensor_copy)
-            attend(1)
             invert_sum(2)
-            scores(3, 0)
             flip_p(2)
             flip_y(1)
+            add_shift(nc.gpsimd, 6, slice(0, 1024))
+            add_shift(nc.gpsimd, 7, slice(0, 1024))
+            flip_w(3, nc.vector.tensor_copy)
             flip_w(4, nc.scalar.copy)
-            flip_w(5, nc.scalar.copy)
             scores(3, 1)
-            add_shift(nc.gpsimd, 10, slice(0, 1024))
-            add_shift(nc.gpsimd, 11, slice(0, 1024))
             project(0, 256, (0, 2), 0)
-            softmax(3)
+            attend(2)
             project(0, 256, (2, 4), 0)
             project(0, 256, (4, 6), 0)
             project(0, 256, (6, 8), 0)
-            attend(2)
-            invert_sum(3)
+            softmax(3)
+            add_shift(nc.gpsimd, 10, slice(0, 1024))
+            add_shift(nc.gpsimd, 11, slice(0, 1024))
             scores(4, 0)
             flip_p(3)
-            flip_y(2)
+            flip_w(5, nc.scalar.copy)
             flip_w(6, nc.scalar.copy)
             flip_w(7, nc.scalar.copy)
-            scores(4, 1)
+            invert_sum(3)
+            flip_y(2)
             add_shift(nc.gpsimd, 12, slice(0, 1024))
             add_shift(nc.gpsimd, 13, slice(0, 1024))
             add_shift(nc.gpsimd, 14, slice(0, 1024))
             add_shift(nc.gpsimd, 15, slice(0, 1024))
             project(0, 256, (8, 10), 0)
-            softmax(4)
-            project(0, 256, (10, 12), 0)
-            project(0, 256, (12, 14), 0)
-            project(0, 256, (14, 16), 0)
+            scores(4, 1)
             attend(3)
-            invert_sum(4)
+            project(0, 256, (10, 12), 0)
+            softmax(4)
+            project(0, 256, (12, 14), 0)
             scores(5, 0)
-            flip_p(4)
+            project(0, 256, (14, 16), 0)
+            invert_sum(4)
             flip_y(3)
+            flip_p(4)
             scores(5, 1)
             project(256, 256, (0, 2), 256)
-            softmax(5)
+            attend(4)
             project(256, 256, (2, 4), 256)
             project(256, 256, (4, 6), 256)
+            softmax(5)
             project(256, 256, (6, 8), 256)
-            attend(4)
-            invert_sum(5)
             scores(6, 0)
             flip_p(5)
+            invert_sum(5)
             flip_y(4)
-            scores(6, 1)
             project(256, 256, (8, 10), 256)
-            softmax(6)
+            scores(6, 1)
+            attend(5)
             project(256, 256, (10, 12), 256)
             project(256, 256, (12, 14), 256)
+            softmax(6)
             project(256, 256, (14, 16), 256)
-            attend(5)
-            invert_sum(6)
+            project(512, 128, (0, 4), 512)
+            project(512, 128, (4, 8), 512)
             scores(7, 0)
             flip_p(6)
             flip_y(5)
+            invert_sum(6)
             scores(7, 1)
-            project(512, 256, (0, 2), 512)
+            project(512, 128, (8, 12), 512)
+            project(512, 128, (12, 16), 512)
+            project(640, 128, (0, 4), 640)
             softmax(7)
-            project(512, 256, (2, 4), 512)
-            project(512, 256, (4, 6), 512)
-            project(512, 256, (6, 8), 512)
+            project(640, 128, (4, 8), 640)
             attend(6)
-            project(512, 256, (8, 10), 512)
-            project(512, 256, (10, 12), 512)
             invert_sum(7)
             flip_p(7)
             flip_y(6)
-            project(512, 256, (12, 14), 512)
-            project(512, 256, (14, 16), 512)
+            project(640, 128, (8, 12), 640)
+            project(640, 128, (12, 16), 640)
             attend(7)
             project(768, 128, (0, 4), 768)
             project(768, 128, (4, 8), 768)
-            project(768, 128, (8, 12), 768)
             flip_y(7)
+            project(768, 128, (8, 12), 768)
             project(768, 128, (12, 16), 768)
             project(896, 128, (0, 4), 896)
             project(896, 128, (4, 8), 896)

@@ -306,26 +306,27 @@ def tile_nonlocalmodule_pa_kernel(tc, theta, phi, g, w_w, w_b, w_bn, x, out):
             scores(2, 0)
             softmax(1)
             attend(0)
-            add_shift(nc.gpsimd, 2, slice(0, 1024))
             invert_sum(1)
             scores(2, 1)
             flip_p(1)
             flip_y(0)
             flip_w(1, nc.vector.tensor_copy)
-            add_shift(nc.gpsimd, 3, slice(0, 1024))
+        with tc.manual_schedule(engines={mybir.EngineType.PE, mybir.EngineType.Activation}):
             scores(3, 0)
             softmax(2)
             attend(1)
-            add_shift(nc.gpsimd, 4, slice(0, 1024))
-            add_shift(nc.gpsimd, 5, slice(0, 1024))
+            add_shift(nc.vector, 2, slice(0, 1024))
+            add_shift(nc.vector, 3, slice(0, 1024))
+            add_shift(nc.vector, 4, slice(0, 1024))
+            add_shift(nc.vector, 5, slice(0, 1024))
             flip_w(2, nc.vector.tensor_copy)
             invert_sum(2)
             flip_p(2)
             flip_y(1)
-            add_shift(nc.gpsimd, 6, slice(0, 1024))
-            add_shift(nc.gpsimd, 7, slice(0, 1024))
             flip_w(3, nc.vector.tensor_copy)
             flip_w(4, nc.scalar.copy)
+            add_shift(nc.vector, 6, slice(0, 1024))
+            add_shift(nc.vector, 7, slice(0, 1024))
             scores(3, 1)
             project(0, 256, (0, 2), 0)
             attend(2)
@@ -333,8 +334,8 @@ def tile_nonlocalmodule_pa_kernel(tc, theta, phi, g, w_w, w_b, w_bn, x, out):
             project(0, 256, (4, 6), 0)
             project(0, 256, (6, 8), 0)
             softmax(3)
-            add_shift(nc.gpsimd, 10, slice(0, 1024))
-            add_shift(nc.gpsimd, 11, slice(0, 1024))
+            add_shift(nc.vector, 10, slice(0, 1024))
+            add_shift(nc.vector, 11, slice(0, 1024))
             scores(4, 0)
             flip_p(3)
             flip_w(5, nc.scalar.copy)
@@ -342,10 +343,10 @@ def tile_nonlocalmodule_pa_kernel(tc, theta, phi, g, w_w, w_b, w_bn, x, out):
             flip_w(7, nc.scalar.copy)
             invert_sum(3)
             flip_y(2)
-            add_shift(nc.gpsimd, 12, slice(0, 1024))
-            add_shift(nc.gpsimd, 13, slice(0, 1024))
-            add_shift(nc.gpsimd, 14, slice(0, 1024))
-            add_shift(nc.gpsimd, 15, slice(0, 1024))
+            add_shift(nc.vector, 12, slice(0, 1024))
+            add_shift(nc.vector, 13, slice(0, 1024))
+            add_shift(nc.vector, 14, slice(0, 1024))
+            add_shift(nc.vector, 15, slice(0, 1024))
             project(0, 256, (8, 10), 0)
             scores(4, 1)
             attend(3)

@@ -24,7 +24,7 @@ OUT_TILES = OUT_CH // P
 HALVES = PIX // BANK
 PAIR = 2 * P
 STORE_TILES = 4
-WARM_PASSES = 6
+WARM_PASSES = 4
 
 FLOPS = 2 * PIX * PIX * EMB * 2 + 2 * OUT_CH * EMB * PIX
 
@@ -81,10 +81,6 @@ def tile_nonlocalmodule_pa_kernel(tc, theta, phi, g, w_w, w_b, w_bn, x, out):
 
         ident = keep.tile([P, P], F32)
         masks.make_identity(nc, ident[:])
-        warm = keep.tile([P, 1], F32)
-        nc.vector.memset(warm[:], 0.0)
-        warm_out = keep.tile([P, 1], F32)
-        nc.scalar.activation(out=warm_out[:], in_=warm[:], func=ACT.Exp)
         zeros = keep.tile([P, BANK], BF16)
         nc.vector.memset(zeros[:], 0.0)
         idle = psum.tile([P, BANK], F32, tag="bank")
@@ -92,12 +88,14 @@ def tile_nonlocalmodule_pa_kernel(tc, theta, phi, g, w_w, w_b, w_bn, x, out):
             nc.tensor.matmul(out=idle[:], lhsT=zeros[:, 0:P], rhs=zeros[:], start=True, stop=True)
 
         gamma, beta, mean, var = (bn_sb[:, v, :] for v in range(4))
-        minus_half = keep.tile([P, OUT_TILES], F32)
-        nc.gpsimd.memset(minus_half[:], -0.5)
         var_eps = keep.tile([P, OUT_TILES], F32)
         nc.vector.tensor_scalar_add(out=var_eps[:], in0=var, scalar1=EPS)
+        std = keep.tile([P, OUT_TILES], F32)
+        nc.scalar.activation(out=std[:], in_=var_eps[:], func=ACT.Sqrt)
+        early_exp = keep.tile([P, 1], F32)
+        nc.scalar.activation(out=early_exp[:], in_=std[:, 0:1], func=ACT.Exp)
         inv_std = keep.tile([P, OUT_TILES], F32)
-        nc.gpsimd.tensor_tensor(out=inv_std[:], in0=var_eps[:], in1=minus_half[:], op=ALU.pow)
+        nc.vector.reciprocal(out=inv_std[:], in_=std[:])
         centred = keep.tile([P, OUT_TILES], F32)
         nc.vector.tensor_tensor(out=centred[:], in0=wb_sb[:], in1=mean, op=ALU.subtract)
         scale = keep.tile([P, OUT_TILES], F32)
@@ -105,7 +103,6 @@ def tile_nonlocalmodule_pa_kernel(tc, theta, phi, g, w_w, w_b, w_bn, x, out):
         scaled = keep.tile([P, OUT_TILES], F32)
         nc.vector.tensor_tensor(out=scaled[:], in0=centred[:], in1=scale[:], op=ALU.mult)
         shift = keep.tile([P, OUT_TILES], F32)
-        nc.vector.tensor_tensor(out=shift[:], in0=scaled[:], in1=beta, op=ALU.add)
 
         result = keep.tile([P, OUT_TILES, PIX], F32)
         g_codes = keep.tile([P, 2 * EMB], U32, align_bytes=64)
@@ -302,7 +299,7 @@ def tile_nonlocalmodule_pa_kernel(tc, theta, phi, g, w_w, w_b, w_bn, x, out):
             scores(1, 1)
             flip_g(1, 0, nc.scalar.copy)
             flip_p(0)
-            flip_w(0, nc.vector.tensor_copy)
+            flip_w(0, nc.scalar.copy)
             scores(2, 0)
             softmax(1)
             attend(0)
@@ -310,23 +307,24 @@ def tile_nonlocalmodule_pa_kernel(tc, theta, phi, g, w_w, w_b, w_bn, x, out):
             scores(2, 1)
             flip_p(1)
             flip_y(0)
-            flip_w(1, nc.vector.tensor_copy)
+            flip_w(1, nc.scalar.copy)
+            nc.vector.tensor_tensor(out=shift[:], in0=scaled[:], in1=beta, op=ALU.add)
         with tc.manual_schedule(engines={mybir.EngineType.PE, mybir.EngineType.Activation}):
             scores(3, 0)
             softmax(2)
             attend(1)
-            add_shift(nc.vector, 2, slice(0, 1024))
-            add_shift(nc.vector, 3, slice(0, 1024))
-            add_shift(nc.vector, 4, slice(0, 1024))
-            add_shift(nc.vector, 5, slice(0, 1024))
+            add_shift(nc.vector, 2, slice(0, 512))
+            add_shift(nc.vector, 3, slice(0, 512))
+            add_shift(nc.vector, 4, slice(0, 512))
+            add_shift(nc.vector, 5, slice(0, 512))
             flip_w(2, nc.vector.tensor_copy)
             invert_sum(2)
             flip_p(2)
             flip_y(1)
             flip_w(3, nc.vector.tensor_copy)
             flip_w(4, nc.scalar.copy)
-            add_shift(nc.vector, 6, slice(0, 1024))
-            add_shift(nc.vector, 7, slice(0, 1024))
+            add_shift(nc.vector, 6, slice(0, 512))
+            add_shift(nc.vector, 7, slice(0, 512))
             scores(3, 1)
             project(0, 256, (0, 2), 0)
             attend(2)
@@ -334,8 +332,8 @@ def tile_nonlocalmodule_pa_kernel(tc, theta, phi, g, w_w, w_b, w_bn, x, out):
             project(0, 256, (4, 6), 0)
             project(0, 256, (6, 8), 0)
             softmax(3)
-            add_shift(nc.vector, 10, slice(0, 1024))
-            add_shift(nc.vector, 11, slice(0, 1024))
+            add_shift(nc.vector, 10, slice(0, 512))
+            add_shift(nc.vector, 11, slice(0, 512))
             scores(4, 0)
             flip_p(3)
             flip_w(5, nc.scalar.copy)
@@ -343,10 +341,10 @@ def tile_nonlocalmodule_pa_kernel(tc, theta, phi, g, w_w, w_b, w_bn, x, out):
             flip_w(7, nc.scalar.copy)
             invert_sum(3)
             flip_y(2)
-            add_shift(nc.vector, 12, slice(0, 1024))
-            add_shift(nc.vector, 13, slice(0, 1024))
-            add_shift(nc.vector, 14, slice(0, 1024))
-            add_shift(nc.vector, 15, slice(0, 1024))
+            add_shift(nc.vector, 12, slice(0, 512))
+            add_shift(nc.vector, 13, slice(0, 512))
+            add_shift(nc.vector, 14, slice(0, 512))
+            add_shift(nc.vector, 15, slice(0, 512))
             project(0, 256, (8, 10), 0)
             scores(4, 1)
             attend(3)
@@ -365,6 +363,12 @@ def tile_nonlocalmodule_pa_kernel(tc, theta, phi, g, w_w, w_b, w_bn, x, out):
             project(256, 256, (4, 6), 256)
             softmax(5)
             project(256, 256, (6, 8), 256)
+            add_shift(nc.vector, 2, slice(512, 1024))
+            add_shift(nc.vector, 3, slice(512, 1024))
+            add_shift(nc.vector, 4, slice(512, 1024))
+            add_shift(nc.vector, 5, slice(512, 1024))
+            add_shift(nc.vector, 6, slice(512, 1024))
+            add_shift(nc.vector, 7, slice(512, 1024))
             scores(6, 0)
             flip_p(5)
             invert_sum(5)
@@ -375,6 +379,12 @@ def tile_nonlocalmodule_pa_kernel(tc, theta, phi, g, w_w, w_b, w_bn, x, out):
             project(256, 256, (10, 12), 256)
             project(256, 256, (12, 14), 256)
             softmax(6)
+            add_shift(nc.vector, 10, slice(512, 1024))
+            add_shift(nc.vector, 11, slice(512, 1024))
+            add_shift(nc.vector, 12, slice(512, 1024))
+            add_shift(nc.vector, 13, slice(512, 1024))
+            add_shift(nc.vector, 14, slice(512, 1024))
+            add_shift(nc.vector, 15, slice(512, 1024))
             project(256, 256, (14, 16), 256)
             project(512, 128, (0, 4), 512)
             project(512, 128, (4, 8), 512)

@@ -24,7 +24,7 @@ OUT_TILES = OUT_CH // P
 HALVES = PIX // BANK
 PAIR = 2 * P
 STORE_TILES = 4
-WARM_PASSES = 4
+WARM_PASSES = 8
 
 FLOPS = 2 * PIX * PIX * EMB * 2 + 2 * OUT_CH * EMB * PIX
 
@@ -57,7 +57,7 @@ def tile_nonlocalmodule_pa_kernel(tc, theta, phi, g, w_w, w_b, w_bn, x, out):
         out_view = out[0].rearrange("(p j) h w -> p j (h w)", j=OUT_TILES)
 
         def load_w(part):
-            rows = slice(part * 4, (part + 1) * 4)
+            rows = slice(part * 2, (part + 1) * 2)
             nc.sync.dma_start(out=w_sb[:, rows, :], in_=w_view[:, rows, :])
 
         def load_x(part):
@@ -68,9 +68,11 @@ def tile_nonlocalmodule_pa_kernel(tc, theta, phi, g, w_w, w_b, w_bn, x, out):
             nc.sync.dma_start(out=g_sb[:, 2 * u : 2 * u + 2, :].rearrange("q e m -> q (e m)"), in_=g_view[:, u, :])
         nc.sync.dma_start(out=theta_sb[:, :, 256:512], in_=theta_view[:, :, 256:512])
         load_w(0)
+        load_w(1)
         load_x(0)
         load_x(1)
-        load_w(1)
+        load_w(2)
+        load_w(3)
         nc.sync.dma_start(out=theta_sb[:, :, 512:1024], in_=theta_view[:, :, 512:1024])
         load_x(2)
         load_x(3)
@@ -81,11 +83,11 @@ def tile_nonlocalmodule_pa_kernel(tc, theta, phi, g, w_w, w_b, w_bn, x, out):
 
         ident = keep.tile([P, P], F32)
         masks.make_identity(nc, ident[:])
-        zeros = keep.tile([P, BANK], BF16)
+        zeros = keep.tile([P, PAIR], BF16)
         nc.vector.memset(zeros[:], 0.0)
         idle = psum.tile([P, BANK], F32, tag="bank")
         for n in range(WARM_PASSES):
-            nc.tensor.matmul(out=idle[:], lhsT=zeros[:, 0:P], rhs=zeros[:], start=True, stop=True)
+            nc.tensor.matmul(out=idle[:, 0:PAIR], lhsT=zeros[:, 0:P], rhs=zeros[:], start=True, stop=True)
 
         gamma, beta, mean, var = (bn_sb[:, v, :] for v in range(4))
         var_eps = keep.tile([P, OUT_TILES], F32)
@@ -93,7 +95,7 @@ def tile_nonlocalmodule_pa_kernel(tc, theta, phi, g, w_w, w_b, w_bn, x, out):
         std = keep.tile([P, OUT_TILES], F32)
         nc.scalar.activation(out=std[:], in_=var_eps[:], func=ACT.Sqrt)
         early_exp = keep.tile([P, 1], F32)
-        nc.scalar.activation(out=early_exp[:], in_=std[:, 0:1], func=ACT.Exp)
+        nc.scalar.activation(out=early_exp[:], in_=std[:, 0:1], func=ACT.Exp, scale=0.0)
         inv_std = keep.tile([P, OUT_TILES], F32)
         nc.vector.reciprocal(out=inv_std[:], in_=std[:])
         centred = keep.tile([P, OUT_TILES], F32)
@@ -158,16 +160,21 @@ def tile_nonlocalmodule_pa_kernel(tc, theta, phi, g, w_w, w_b, w_bn, x, out):
                 )
 
         def score_max(i, half):
-            negated = stage.tile([P, BANK], BF16, name="negated")
             neg_max[i, half] = stage.tile([P, 1], F32, name="neg_max%d" % half)
+            if half == 0:
+                nc.vector.tensor_reduce(
+                    out=neg_max[i, 0][:], in_=score[i, 0][:], axis=AXIS.X, op=ALU.max, negate=True
+                )
+                return
+            negated = stage.tile([P, BANK], BF16, name="negated")
             nc.vector.tensor_scalar(
                 out=negated[:],
-                in0=score[i, half][:],
+                in0=score[i, 1][:],
                 scalar1=-1.0,
-                scalar2=None if half == 0 else neg_max[i, 0][:, 0:1],
+                scalar2=neg_max[i, 0][:, 0:1],
                 op0=ALU.mult,
                 op1=ALU.min,
-                accum_out=neg_max[i, half][:, 0:1],
+                accum_out=neg_max[i, 1][:, 0:1],
             )
 
         def scores(i, half):
@@ -235,7 +242,7 @@ def tile_nonlocalmodule_pa_kernel(tc, theta, phi, g, w_w, w_b, w_bn, x, out):
                     op1=ALU.add,
                 )
 
-        def project(start, width, tiles, store_from=None):
+        def project(start, width, tiles):
             cols = slice(start, start + width)
             per_bank = BANK // width
             for j0 in range(tiles[0], tiles[1], per_bank):
@@ -279,10 +286,11 @@ def tile_nonlocalmodule_pa_kernel(tc, theta, phi, g, w_w, w_b, w_bn, x, out):
                         op=ALU.add,
                     )
                 last = j0 + per_bank
-                if store_from is not None and last % STORE_TILES == 0:
-                    stored = slice(last - STORE_TILES, last)
-                    done = slice(store_from, start + width)
-                    nc.sync.dma_start(out=out_view[:, stored, done], in_=result[:, stored, done])
+                if last % STORE_TILES == 0:
+                    store_tiles = STORE_TILES // 2 if start == PIX - P else STORE_TILES
+                    for j in range(last - STORE_TILES, last, store_tiles):
+                        stored = slice(j, j + store_tiles)
+                        nc.sync.dma_start(out=out_view[:, stored, cols], in_=result[:, stored, cols])
 
         with tc.manual_schedule():
             for k in range(EMB_TILES):
@@ -326,11 +334,11 @@ def tile_nonlocalmodule_pa_kernel(tc, theta, phi, g, w_w, w_b, w_bn, x, out):
             add_shift(nc.vector, 6, slice(0, 512))
             add_shift(nc.vector, 7, slice(0, 512))
             scores(3, 1)
-            project(0, 256, (0, 2), 0)
+            project(0, 256, (0, 2))
             attend(2)
-            project(0, 256, (2, 4), 0)
-            project(0, 256, (4, 6), 0)
-            project(0, 256, (6, 8), 0)
+            project(0, 256, (2, 4))
+            project(0, 256, (4, 6))
+            project(0, 256, (6, 8))
             softmax(3)
             add_shift(nc.vector, 10, slice(0, 512))
             add_shift(nc.vector, 11, slice(0, 512))
@@ -345,24 +353,24 @@ def tile_nonlocalmodule_pa_kernel(tc, theta, phi, g, w_w, w_b, w_bn, x, out):
             add_shift(nc.vector, 13, slice(0, 512))
             add_shift(nc.vector, 14, slice(0, 512))
             add_shift(nc.vector, 15, slice(0, 512))
-            project(0, 256, (8, 10), 0)
+            project(0, 256, (8, 10))
             scores(4, 1)
             attend(3)
-            project(0, 256, (10, 12), 0)
+            project(0, 256, (10, 12))
             softmax(4)
-            project(0, 256, (12, 14), 0)
+            project(0, 256, (12, 14))
             scores(5, 0)
-            project(0, 256, (14, 16), 0)
+            project(0, 256, (14, 16))
             invert_sum(4)
             flip_y(3)
             flip_p(4)
             scores(5, 1)
-            project(256, 256, (0, 2), 256)
+            project(256, 256, (0, 2))
             attend(4)
-            project(256, 256, (2, 4), 256)
-            project(256, 256, (4, 6), 256)
+            project(256, 256, (2, 4))
+            project(256, 256, (4, 6))
             softmax(5)
-            project(256, 256, (6, 8), 256)
+            project(256, 256, (6, 8))
             add_shift(nc.vector, 2, slice(512, 1024))
             add_shift(nc.vector, 3, slice(512, 1024))
             add_shift(nc.vector, 4, slice(512, 1024))
@@ -373,11 +381,11 @@ def tile_nonlocalmodule_pa_kernel(tc, theta, phi, g, w_w, w_b, w_bn, x, out):
             flip_p(5)
             invert_sum(5)
             flip_y(4)
-            project(256, 256, (8, 10), 256)
+            project(256, 256, (8, 10))
             scores(6, 1)
             attend(5)
-            project(256, 256, (10, 12), 256)
-            project(256, 256, (12, 14), 256)
+            project(256, 256, (10, 12))
+            project(256, 256, (12, 14))
             softmax(6)
             add_shift(nc.vector, 10, slice(512, 1024))
             add_shift(nc.vector, 11, slice(512, 1024))
@@ -385,32 +393,32 @@ def tile_nonlocalmodule_pa_kernel(tc, theta, phi, g, w_w, w_b, w_bn, x, out):
             add_shift(nc.vector, 13, slice(512, 1024))
             add_shift(nc.vector, 14, slice(512, 1024))
             add_shift(nc.vector, 15, slice(512, 1024))
-            project(256, 256, (14, 16), 256)
-            project(512, 128, (0, 4), 512)
-            project(512, 128, (4, 8), 512)
+            project(256, 256, (14, 16))
+            project(512, 128, (0, 4))
+            project(512, 128, (4, 8))
             scores(7, 0)
             flip_p(6)
             flip_y(5)
             invert_sum(6)
             scores(7, 1)
-            project(512, 128, (8, 12), 512)
-            project(512, 128, (12, 16), 512)
-            project(640, 128, (0, 4), 640)
+            project(512, 128, (8, 12))
+            project(512, 128, (12, 16))
+            project(640, 128, (0, 4))
             softmax(7)
-            project(640, 128, (4, 8), 640)
+            project(640, 128, (4, 8))
             attend(6)
             invert_sum(7)
             flip_p(7)
             flip_y(6)
-            project(640, 128, (8, 12), 640)
-            project(640, 128, (12, 16), 640)
+            project(640, 128, (8, 12))
+            project(640, 128, (12, 16))
             attend(7)
-            project(768, 128, (0, 4), 768)
-            project(768, 128, (4, 8), 768)
+            project(768, 128, (0, 4))
+            project(768, 128, (4, 8))
             flip_y(7)
-            project(768, 128, (8, 12), 768)
-            project(768, 128, (12, 16), 768)
-            project(896, 128, (0, 4), 896)
-            project(896, 128, (4, 8), 896)
-            project(896, 128, (8, 12), 896)
-            project(896, 128, (12, 16), 896)
+            project(768, 128, (8, 12))
+            project(768, 128, (12, 16))
+            project(896, 128, (0, 4))
+            project(896, 128, (4, 8))
+            project(896, 128, (8, 12))
+            project(896, 128, (12, 16))

@@ -371,12 +371,12 @@ def tile_nonlocalmodule_pa_kernel(tc, theta, phi, g, w_w, w_b, w_bn, x, out):
             project(256, 256, (4, 6))
             softmax(5)
             project(256, 256, (6, 8))
-            add_shift(nc.vector, 2, slice(512, 1024))
-            add_shift(nc.vector, 3, slice(512, 1024))
-            add_shift(nc.vector, 4, slice(512, 1024))
-            add_shift(nc.vector, 5, slice(512, 1024))
-            add_shift(nc.vector, 6, slice(512, 1024))
-            add_shift(nc.vector, 7, slice(512, 1024))
+            add_shift(nc.gpsimd, 2, slice(512, 1024))
+            add_shift(nc.gpsimd, 3, slice(512, 1024))
+            add_shift(nc.gpsimd, 4, slice(512, 1024))
+            add_shift(nc.gpsimd, 5, slice(512, 1024))
+            add_shift(nc.gpsimd, 6, slice(512, 1024))
+            add_shift(nc.gpsimd, 7, slice(512, 1024))
             scores(6, 0)
             flip_p(5)
             invert_sum(5)
@@ -387,12 +387,12 @@ def tile_nonlocalmodule_pa_kernel(tc, theta, phi, g, w_w, w_b, w_bn, x, out):
             project(256, 256, (10, 12))
             project(256, 256, (12, 14))
             softmax(6)
-            add_shift(nc.vector, 10, slice(512, 1024))
-            add_shift(nc.vector, 11, slice(512, 1024))
-            add_shift(nc.vector, 12, slice(512, 1024))
-            add_shift(nc.vector, 13, slice(512, 1024))
-            add_shift(nc.vector, 14, slice(512, 1024))
-            add_shift(nc.vector, 15, slice(512, 1024))
+            add_shift(nc.gpsimd, 10, slice(512, 1024))
+            add_shift(nc.gpsimd, 11, slice(512, 1024))
+            add_shift(nc.gpsimd, 12, slice(512, 1024))
+            add_shift(nc.gpsimd, 13, slice(512, 1024))
+            add_shift(nc.gpsimd, 14, slice(512, 1024))
+            add_shift(nc.gpsimd, 15, slice(512, 1024))
             project(256, 256, (14, 16))
             project(512, 128, (0, 4))
             project(512, 128, (4, 8))

@@ -296,8 +296,8 @@ def tile_nonlocalmodule_pa_kernel(tc, theta, phi, g, w_w, w_b, w_bn, x, out):
             for k in range(EMB_TILES):
                 for half in range(HALVES):
                     score_passes(0, half, (k,))
-            for half in range(HALVES):
-                score_max(0, half)
+            score_max(0, 0)
+            score_max(0, 1)
             flip_g(0, 0, nc.scalar.copy)
             softmax(0)
             invert_sum(0)
@@ -317,7 +317,7 @@ def tile_nonlocalmodule_pa_kernel(tc, theta, phi, g, w_w, w_b, w_bn, x, out):
             flip_y(0)
             flip_w(1, nc.scalar.copy)
             nc.vector.tensor_tensor(out=shift[:], in0=scaled[:], in1=beta, op=ALU.add)
-        with tc.manual_schedule(engines={mybir.EngineType.PE, mybir.EngineType.Activation}):
+        with tc.manual_schedule(engines={mybir.EngineType.PE, mybir.EngineType.Activation, mybir.EngineType.Pool}):
             scores(3, 0)
             softmax(2)
             attend(1)
@@ -335,6 +335,9 @@ def tile_nonlocalmodule_pa_kernel(tc, theta, phi, g, w_w, w_b, w_bn, x, out):
             add_shift(nc.vector, 7, slice(0, 512))
             scores(3, 1)
             project(0, 256, (0, 2))
+            add_shift(nc.gpsimd, 2, slice(512, 1024))
+            add_shift(nc.gpsimd, 3, slice(512, 1024))
+            add_shift(nc.gpsimd, 4, slice(512, 1024))
             attend(2)
             project(0, 256, (2, 4))
             project(0, 256, (4, 6))
@@ -354,45 +357,42 @@ def tile_nonlocalmodule_pa_kernel(tc, theta, phi, g, w_w, w_b, w_bn, x, out):
             add_shift(nc.vector, 14, slice(0, 512))
             add_shift(nc.vector, 15, slice(0, 512))
             project(0, 256, (8, 10))
+            add_shift(nc.gpsimd, 5, slice(512, 1024))
+            add_shift(nc.gpsimd, 6, slice(512, 1024))
+            add_shift(nc.gpsimd, 7, slice(512, 1024))
             scores(4, 1)
             attend(3)
             project(0, 256, (10, 12))
             softmax(4)
             project(0, 256, (12, 14))
-            scores(5, 0)
             project(0, 256, (14, 16))
+            scores(5, 0)
             invert_sum(4)
             flip_y(3)
             flip_p(4)
             scores(5, 1)
             project(256, 256, (0, 2))
+            add_shift(nc.gpsimd, 10, slice(512, 1024))
+            add_shift(nc.gpsimd, 11, slice(512, 1024))
+            add_shift(nc.gpsimd, 12, slice(512, 1024))
             attend(4)
             project(256, 256, (2, 4))
             project(256, 256, (4, 6))
             softmax(5)
             project(256, 256, (6, 8))
-            add_shift(nc.gpsimd, 2, slice(512, 1024))
-            add_shift(nc.gpsimd, 3, slice(512, 1024))
-            add_shift(nc.gpsimd, 4, slice(512, 1024))
-            add_shift(nc.gpsimd, 5, slice(512, 1024))
-            add_shift(nc.gpsimd, 6, slice(512, 1024))
-            add_shift(nc.gpsimd, 7, slice(512, 1024))
+            project(256, 256, (8, 10))
+            add_shift(nc.gpsimd, 13, slice(512, 1024))
+            add_shift(nc.gpsimd, 14, slice(512, 1024))
+            add_shift(nc.gpsimd, 15, slice(512, 1024))
             scores(6, 0)
             flip_p(5)
             invert_sum(5)
             flip_y(4)
-            project(256, 256, (8, 10))
+            project(256, 256, (10, 12))
             scores(6, 1)
             attend(5)
-            project(256, 256, (10, 12))
             project(256, 256, (12, 14))
             softmax(6)
-            add_shift(nc.gpsimd, 10, slice(512, 1024))
-            add_shift(nc.gpsimd, 11, slice(512, 1024))
-            add_shift(nc.gpsimd, 12, slice(512, 1024))
-            add_shift(nc.gpsimd, 13, slice(512, 1024))
-            add_shift(nc.gpsimd, 14, slice(512, 1024))
-            add_shift(nc.gpsimd, 15, slice(512, 1024))
             project(256, 256, (14, 16))
             project(512, 128, (0, 4))
             project(512, 128, (4, 8))

from contextlib import ExitStack

import concourse.masks as masks
import concourse.mybir as mybir

BF16 = mybir.dt.bfloat16
F32 = mybir.dt.float32
U32 = mybir.dt.uint32
U8 = mybir.dt.uint8
FP8X4 = mybir.dt.float8_e4m3fn_x4
ALU = mybir.AluOpType
ACT = mybir.ActivationFunctionType
AXIS = mybir.AxisListType

P = 128
EMB = 512
PIX = 1024
OUT_CH = 2048
EPS = 1e-5
BANK = 512
EMB_TILES = EMB // P
ROW_TILES = PIX // P
OUT_TILES = OUT_CH // P
HALVES = PIX // BANK
PAIR = 2 * P
STORE_TILES = 4
WARM_PASSES = 8

FLOPS = 2 * PIX * PIX * EMB * 2 + 2 * OUT_CH * EMB * PIX


def by_scalar(j, width):
    return j % 8 < 2


def tile_nonlocalmodule_pa_kernel(tc, theta, phi, g, w_w, w_b, w_bn, x, out):
    nc = tc.nc
    with ExitStack() as ctx:
        keep = ctx.enter_context(tc.tile_pool(name="keep", bufs=1))
        stage = ctx.enter_context(tc.tile_pool(name="stage", bufs=4))
        score_psum = ctx.enter_context(tc.psum_pool(name="score_psum", bufs=3))
        psum = ctx.enter_context(tc.psum_pool(name="psum", bufs=5))

        theta_view = theta[0].rearrange("(p k) n -> p k n", k=EMB_TILES)
        phi_view = phi[0].rearrange("(p k) m -> p k m", k=EMB_TILES)
        theta_sb = keep.tile([P, EMB_TILES, PIX], BF16)
        phi_sb = keep.tile([P, EMB_TILES, PIX], BF16)
        nc.sync.dma_start(out=theta_sb[:, :, 0:PAIR], in_=theta_view[:, :, 0:PAIR])
        for k in range(EMB_TILES):
            nc.sync.dma_start(out=phi_sb[:, k, :], in_=phi_view[:, k, :])
        g_sb = keep.tile([P, EMB_TILES, PIX], BF16)
        g_view = g[0].rearrange("(u q e) m -> q u (e m)", u=2, e=2)
        w_sb = keep.tile([P, OUT_TILES // 2, 2 * EMB], BF16)
        w_view = w_w.rearrange("(p a b) c -> p a (b c)", a=OUT_TILES // 2, b=2)
        x_sb = keep.tile([P, OUT_TILES, PIX], BF16)
        x_view = x[0].rearrange("(p j) h w -> p j (h w)", j=OUT_TILES)
        out_view = out[0].rearrange("(p j) h w -> p j (h w)", j=OUT_TILES)

        def load_w(part):
            rows = slice(part * 2, (part + 1) * 2)
            nc.sync.dma_start(out=w_sb[:, rows, :], in_=w_view[:, rows, :])

        def load_x(part):
            rows = slice(part * 4, (part + 1) * 4)
            nc.sync.dma_start(out=x_sb[:, rows, :], in_=x_view[:, rows, :])

        for u in range(2):
            nc.sync.dma_start(out=g_sb[:, 2 * u : 2 * u + 2, :].rearrange("q e m -> q (e m)"), in_=g_view[:, u, :])
        nc.sync.dma_start(out=theta_sb[:, :, 256:512], in_=theta_view[:, :, 256:512])
        load_w(0)
        load_w(1)
        load_x(0)
        load_x(1)
        load_w(2)
        load_w(3)
        nc.sync.dma_start(out=theta_sb[:, :, 512:1024], in_=theta_view[:, :, 512:1024])
        load_x(2)
        load_x(3)
        bn_sb = keep.tile([P, 4, OUT_TILES], BF16)
        nc.scalar.dma_start(out=bn_sb[:], in_=w_bn.rearrange("v (p j) -> p v j", j=OUT_TILES))
        wb_sb = keep.tile([P, OUT_TILES], BF16)
        nc.scalar.dma_start(out=wb_sb[:], in_=w_b.rearrange("(p j) -> p j", j=OUT_TILES))

        ident = keep.tile([P, P], F32)
        masks.make_identity(nc, ident[:])
        zeros = keep.tile([P, PAIR], BF16)
        nc.vector.memset(zeros[:], 0.0)
        idle = psum.tile([P, BANK], F32, tag="bank")
        for n in range(WARM_PASSES):
            nc.tensor.matmul(out=idle[:, 0:PAIR], lhsT=zeros[:, 0:P], rhs=zeros[:], start=True, stop=True)

        gamma, beta, mean, var = (bn_sb[:, v, :] for v in range(4))
        var_eps = keep.tile([P, OUT_TILES], F32)
        nc.vector.tensor_scalar_add(out=var_eps[:], in0=var, scalar1=EPS)
        std = keep.tile([P, OUT_TILES], F32)
        nc.scalar.activation(out=std[:], in_=var_eps[:], func=ACT.Sqrt)
        early_exp = keep.tile([P, 1], F32)
        nc.scalar.activation(out=early_exp[:], in_=std[:, 0:1], func=ACT.Exp, scale=0.0)
        inv_std = keep.tile([P, OUT_TILES], F32)
        nc.vector.reciprocal(out=inv_std[:], in_=std[:])
        centred = keep.tile([P, OUT_TILES], F32)
        nc.vector.tensor_tensor(out=centred[:], in0=wb_sb[:], in1=mean, op=ALU.subtract)
        scale = keep.tile([P, OUT_TILES], F32)
        nc.vector.tensor_tensor(out=scale[:], in0=gamma, in1=inv_std[:], op=ALU.mult)
        scaled = keep.tile([P, OUT_TILES], F32)
        nc.vector.tensor_tensor(out=scaled[:], in0=centred[:], in1=scale[:], op=ALU.mult)
        shift = keep.tile([P, OUT_TILES], F32)

        result = keep.tile([P, OUT_TILES, PIX], F32)
        g_codes = keep.tile([P, 2 * EMB], U32, align_bytes=64)
        g_scales = keep.tile([P, 2 * EMB], U8, align_bytes=64)
        w_codes = keep.tile([P, OUT_CH], U32, align_bytes=64)
        w_scales = keep.tile([P, OUT_CH], U8, align_bytes=64)
        y_codes = keep.tile([P, PIX], U32, align_bytes=64)
        y_scales = keep.tile([P, PIX], U8, align_bytes=64)

        def flip_to_mx(blocks, codes, scales, copy, order="a r u"):
            groups = len(blocks) // 2
            width = len(blocks) * P
            flipped = psum.tile([P, width], F32, tag="bank", name="flipped")
            for b, block in enumerate(blocks):
                nc.tensor.transpose(flipped[:, b * P : (b + 1) * P], block, ident[:])
            grouped = stage.tile([P, 2 * width], BF16, align_bytes=64, name="grouped", tag="grouped%d" % groups)
            copy(
                out=grouped[:].bitcast(F32).rearrange("q (%s) -> q %s" % (order, order), a=groups, u=2),
                in_=flipped[:].rearrange("q (a u r) -> q %s" % order, a=groups, u=2),
            )
            nc.vector.quantize_mx(out=codes.bitcast(FP8X4), scales=scales, in_=grouped[:])

        def words_of(rows, count):
            words = rows.bitcast(F32)
            return [words[:, b * P : (b + 1) * P] for b in range(count)]

        def flip_g(a, pair, copy):
            blocks = []
            for t in (2 * pair, 2 * pair + 1):
                blocks.extend(words_of(g_sb[:, t, :], 4)[2 * a : 2 * a + 2])
            cols = slice(a * EMB + pair * 2 * P, a * EMB + (pair + 1) * 2 * P)
            flip_to_mx(blocks, g_codes[:, cols], g_scales[:, cols], copy, "r a u")

        def flip_w(pair, copy):
            cols = slice(pair * 2 * P, (pair + 1) * 2 * P)
            flip_to_mx(words_of(w_sb[:, pair, :], 4), w_codes[:, cols], w_scales[:, cols], copy)

        score, neg_max, prob, half_sum, inv_sum = {}, {}, {}, {}, {}
        p_codes, p_scales, y_rows = {}, {}, {}

        def score_passes(i, half, slots):
            queries = slice(i * P, (i + 1) * P)
            keys = slice(half * BANK, (half + 1) * BANK)
            if slots[0] == 0:
                score[i, half] = score_psum.tile([P, BANK], F32, name="score")
            for k in slots:
                nc.tensor.matmul(
                    out=score[i, half][:],
                    lhsT=theta_sb[:, k, queries],
                    rhs=phi_sb[:, k, keys],
                    start=(k == 0),
                    stop=(k == EMB_TILES - 1),
                )

        def score_max(i, half):
            neg_max[i, half] = stage.tile([P, 1], F32, name="neg_max%d" % half)
            if half == 0:
                nc.vector.tensor_reduce(
                    out=neg_max[i, 0][:], in_=score[i, 0][:], axis=AXIS.X, op=ALU.max, negate=True
                )
                return
            negated = stage.tile([P, BANK], BF16, name="negated")
            nc.vector.tensor_scalar(
                out=negated[:],
                in0=score[i, 1][:],
                scalar1=-1.0,
                scalar2=neg_max[i, 0][:, 0:1],
                op0=ALU.mult,
                op1=ALU.min,
                accum_out=neg_max[i, 1][:, 0:1],
            )

        def scores(i, half):
            score_passes(i, half, range(EMB_TILES))
            score_max(i, half)

        def softmax(i):
            prob[i] = stage.tile([P, PIX], BF16, name="prob")
            half_sum[i] = stage.tile([P, HALVES], F32, name="half_sum")
            for half in range(HALVES):
                keys = slice(half * BANK, (half + 1) * BANK)
                nc.scalar.activation(
                    out=prob[i][:, keys],
                    in_=score[i, half][:],
                    func=ACT.Exp,
                    bias=neg_max[i, 1][:, 0:1],
                    scale=1.0,
                    accum_out=half_sum[i][:, half : half + 1],
                )

        def invert_sum(i):
            row_sum = stage.tile([P, 1], F32)
            nc.vector.tensor_reduce(out=row_sum[:], in_=half_sum[i][:], axis=AXIS.X, op=ALU.add)
            inv_sum[i] = stage.tile([P, 1], F32, name="inv_sum")
            nc.vector.reciprocal(out=inv_sum[i][:], in_=row_sum[:])

        def flip_p(i):
            p_codes[i] = stage.tile([P, 2 * P], U32, align_bytes=64, name="p_codes")
            p_scales[i] = stage.tile([P, 2 * P], U8, align_bytes=64, name="p_scales")
            flip_to_mx(words_of(prob[i][:], 4), p_codes[i][:], p_scales[i][:], nc.scalar.copy)

        def attend(i):
            y_ps = psum.tile([P, EMB], F32, tag="bank")
            for a in range(2):
                p_cols = slice(a * P, (a + 1) * P)
                g_cols = slice(a * EMB, (a + 1) * EMB)
                nc.tensor.matmul_mx(
                    out=y_ps[:],
                    lhsT=p_codes[i][:, p_cols].bitcast(FP8X4),
                    lhsT_scale=p_scales[i][:, p_cols],
                    rhs=g_codes[:, g_cols].bitcast(FP8X4),
                    rhs_scale=g_scales[:, g_cols],
                    start=(a == 0),
                    stop=(a == 1),
                )
            y_rows[i] = stage.tile([P, EMB], BF16, name="y_rows")
            nc.scalar.activation(out=y_rows[i][:], in_=y_ps[:], func=ACT.Copy, scale=inv_sum[i][:, 0:1])

        def flip_y(i):
            cols = slice(i * P, (i + 1) * P)
            flip_to_mx(words_of(y_rows[i][:], 2), y_codes[:, cols], y_scales[:, cols], nc.scalar.copy)

        def add_shift(engine, j, cols):
            if engine is nc.scalar:
                nc.scalar.activation(
                    out=result[:, j, cols], in_=x_sb[:, j, cols], func=ACT.Identity, bias=shift[:, j : j + 1], scale=1.0
                )
            else:
                engine.tensor_scalar(
                    out=result[:, j, cols],
                    in0=x_sb[:, j, cols],
                    scalar1=1.0,
                    scalar2=shift[:, j : j + 1],
                    op0=ALU.mult,
                    op1=ALU.add,
                )

        def project(start, width, tiles):
            cols = slice(start, start + width)
            per_bank = BANK // width
            for j0 in range(tiles[0], tiles[1], per_bank):
                z_ps = psum.tile([P, per_bank, width], F32, tag="bank", name="z_ps")
                for b in range(per_bank):
                    w_cols = slice((j0 + b) * P, (j0 + b + 1) * P)
                    nc.tensor.matmul_mx(
                        out=z_ps[:, b, :],
                        lhsT=w_codes[:, w_cols].bitcast(FP8X4),
                        lhsT_scale=w_scales[:, w_cols],
                        rhs=y_codes[:, cols].bitcast(FP8X4),
                        rhs_scale=y_scales[:, cols],
                        start=True,
                        stop=True,
                    )
                for b in range(per_bank):
                    j = j0 + b
                    if by_scalar(j, width):
                        nc.scalar.activation(
                            out=result[:, j, cols],
                            in_=z_ps[:, b, :],
                            func=ACT.Identity,
                            bias=shift[:, j : j + 1],
                            scale=scale[:, j : j + 1],
                        )
                    else:
                        nc.vector.scalar_tensor_tensor(
                            out=result[:, j, cols],
                            in0=z_ps[:, b, :],
                            scalar=scale[:, j : j + 1],
                            in1=result[:, j, cols],
                            op0=ALU.mult,
                            op1=ALU.add,
                        )
                if by_scalar(j0, width):
                    bank_tiles = slice(j0, j0 + 2)
                    nc.gpsimd.tensor_tensor(
                        out=result[:, bank_tiles, cols],
                        in0=result[:, bank_tiles, cols],
                        in1=x_sb[:, bank_tiles, cols],
                        op=ALU.add,
                    )
                last = j0 + per_bank
                if last % STORE_TILES == 0:
                    store_tiles = STORE_TILES // 2 if start == PIX - P else STORE_TILES
                    for j in range(last - STORE_TILES, last, store_tiles):
                        stored = slice(j, j + store_tiles)
                        nc.sync.dma_start(out=out_view[:, stored, cols], in_=result[:, stored, cols])

        with tc.manual_schedule():
            for k in range(EMB_TILES):
                for half in range(HALVES):
                    score_passes(0, half, (k,))
            score_max(0, 0)
            score_max(0, 1)
            flip_g(0, 0, nc.scalar.copy)
            softmax(0)
            invert_sum(0)
            scores(1, 0)
            flip_g(0, 1, nc.scalar.copy)
            flip_g(1, 1, nc.scalar.copy)
            scores(1, 1)
            flip_g(1, 0, nc.scalar.copy)
            flip_p(0)
            flip_w(0, nc.scalar.copy)
            scores(2, 0)
            softmax(1)
            attend(0)
            invert_sum(1)
            scores(2, 1)
            flip_p(1)
            flip_y(0)
            flip_w(1, nc.scalar.copy)
            nc.vector.tensor_tensor(out=shift[:], in0=scaled[:], in1=beta, op=ALU.add)
        with tc.manual_schedule(engines={mybir.EngineType.PE, mybir.EngineType.Activation, mybir.EngineType.Pool}):
            scores(3, 0)
            softmax(2)
            attend(1)
            add_shift(nc.vector, 2, slice(0, 512))
            add_shift(nc.vector, 3, slice(0, 512))
            add_shift(nc.vector, 4, slice(0, 512))
            add_shift(nc.vector, 5, slice(0, 512))
            flip_w(2, nc.vector.tensor_copy)
            invert_sum(2)
            flip_p(2)
            flip_y(1)
            flip_w(3, nc.vector.tensor_copy)
            flip_w(4, nc.scalar.copy)
            add_shift(nc.vector, 6, slice(0, 512))
            add_shift(nc.vector, 7, slice(0, 512))
            scores(3, 1)
            project(0, 256, (0, 2))
            add_shift(nc.gpsimd, 2, slice(512, 1024))
            add_shift(nc.gpsimd, 3, slice(512, 1024))
            add_shift(nc.gpsimd, 4, slice(512, 1024))
            attend(2)
            project(0, 256, (2, 4))
            project(0, 256, (4, 6))
            project(0, 256, (6, 8))
            softmax(3)
            add_shift(nc.vector, 10, slice(0, 512))
            add_shift(nc.vector, 11, slice(0, 512))
            scores(4, 0)
            flip_p(3)
            flip_w(5, nc.scalar.copy)
            flip_w(6, nc.scalar.copy)
            flip_w(7, nc.scalar.copy)
            invert_sum(3)
            flip_y(2)
            add_shift(nc.vector, 12, slice(0, 512))
            add_shift(nc.vector, 13, slice(0, 512))
            add_shift(nc.vector, 14, slice(0, 512))
            add_shift(nc.vector, 15, slice(0, 512))
            project(0, 256, (8, 10))
            add_shift(nc.gpsimd, 5, slice(512, 1024))
            add_shift(nc.gpsimd, 6, slice(512, 1024))
            add_shift(nc.gpsimd, 7, slice(512, 1024))
            scores(4, 1)
            attend(3)
            project(0, 256, (10, 12))
            softmax(4)
            project(0, 256, (12, 14))
            project(0, 256, (14, 16))
            scores(5, 0)
            invert_sum(4)
            flip_y(3)
            flip_p(4)
            scores(5, 1)
            project(256, 256, (0, 2))
            add_shift(nc.gpsimd, 10, slice(512, 1024))
            add_shift(nc.gpsimd, 11, slice(512, 1024))
            add_shift(nc.gpsimd, 12, slice(512, 1024))
            attend(4)
            project(256, 256, (2, 4))
            project(256, 256, (4, 6))
            softmax(5)
            project(256, 256, (6, 8))
            project(256, 256, (8, 10))
            add_shift(nc.gpsimd, 13, slice(512, 1024))
            add_shift(nc.gpsimd, 14, slice(512, 1024))
            add_shift(nc.gpsimd, 15, slice(512, 1024))
            scores(6, 0)
            flip_p(5)
            invert_sum(5)
            flip_y(4)
            project(256, 256, (10, 12))
            scores(6, 1)
            attend(5)
            project(256, 256, (12, 14))
            softmax(6)
            project(256, 256, (14, 16))
            project(512, 128, (0, 4))
            project(512, 128, (4, 8))
            scores(7, 0)
            flip_p(6)
            flip_y(5)
            invert_sum(6)
            scores(7, 1)
            project(512, 128, (8, 12))
            project(512, 128, (12, 16))
            project(640, 128, (0, 4))
            softmax(7)
            project(640, 128, (4, 8))
            attend(6)
            invert_sum(7)
            flip_p(7)
            flip_y(6)
            project(640, 128, (8, 12))
            project(640, 128, (12, 16))
            attend(7)
            project(768, 128, (0, 4))
            project(768, 128, (4, 8))
            flip_y(7)
            project(768, 128, (8, 12))
            project(768, 128, (12, 16))
            project(896, 128, (0, 4))
            project(896, 128, (4, 8))
            project(896, 128, (8, 12))
            project(896, 128, (12, 16))
